import numpy as np
import ml_dtypes


def mxq(x, axis, fmt="e4m3"):
    dtype, down = {"e4m3": (ml_dtypes.float8_e4m3fn, 7), "e5m2": (ml_dtypes.float8_e5m2, 14)}[fmt]
    v = np.moveaxis(np.asarray(x, np.float32).astype(ml_dtypes.bfloat16).astype(np.float64), axis, -1)
    blocks = v.reshape(v.shape[:-1] + (-1, 32))
    amax = np.abs(blocks).max(-1, keepdims=True)
    byte = np.maximum(np.where(amax > 0, np.frexp(amax)[1] - 1 + 127, 0) - down, 1)
    scale = np.exp2(byte - 127.0)
    codes = (blocks / scale).astype(np.float32).astype(dtype).astype(np.float64)
    return np.moveaxis((codes * scale).reshape(v.shape), -1, axis)


WIDE = False


def mx_kscale(k):
    if not WIDE:
        return np.ones(k)
    levels = np.array([10, -10, 5, -5, 0])
    a = np.random.permutation(np.resize(levels, k // 512 * 4)).reshape(k // 512, 4)
    idx = np.arange(k)
    return np.exp2(a[idx // 512, idx % 128 // 32])


BF16 = ml_dtypes.bfloat16


def bf(x):
    return np.asarray(x, np.float32).astype(BF16)


def f64(x):
    return np.asarray(x).astype(np.float64)


B, S, H, HD, DX, NW = 8, 512, 1, 128, 1024, 4
D = H * HD


def split_heads(t):
    return t.reshape(B, S, H, HD).transpose(0, 2, 1, 3)


def merge_heads(t):
    return t.transpose(0, 2, 1, 3).reshape(B, S, D)


def setup_inputs():
    s = mx_kscale(DX)
    w = 1.0 / np.sqrt(DX)
    return {
        "x_real": bf(np.random.standard_normal((B, S, DX)) * s),
        "x_imag": bf(np.random.standard_normal((B, S, DX)) * s),
        "q_zeta_r": bf(np.random.standard_normal((B, H, S, HD)) * 1.2),
        "q_zeta_i": bf(np.random.standard_normal((B, H, S, HD)) * 1.2),
        "k_zeta_r": bf(np.random.standard_normal((B, H, S, HD)) * 1.2),
        "k_zeta_i": bf(np.random.standard_normal((B, H, S, HD)) * 1.2),
        "wv_r": bf(np.random.standard_normal((D, DX)) * w / s),
        "wv_i": bf(np.random.standard_normal((D, DX)) * w / s),
        "bv_r": bf(np.random.standard_normal(D) * 0.3),
        "bv_i": bf(np.random.standard_normal(D) * 0.3),
    }


def reference(x_real, x_imag, q_zeta_r, q_zeta_i, k_zeta_r, k_zeta_i, wv_r, wv_i, bv_r, bv_i):
    xr = mxq(f64(x_real), 2, "e4m3")
    xi = mxq(f64(x_imag), 2, "e4m3")
    wr = mxq(f64(wv_r), 1, "e4m3")
    wi = mxq(f64(wv_i), 1, "e4m3")
    v_r = (xr @ wr.T) - (xi @ wi.T) + f64(bv_r)
    v_i = (xr @ wi.T) + (xi @ wr.T) + f64(bv_i)
    qr, qi = f64(q_zeta_r), f64(q_zeta_i)
    krt = f64(k_zeta_r).transpose(0, 1, 3, 2)
    kit = f64(k_zeta_i).transpose(0, 1, 3, 2)
    s_r = (qr @ krt - qi @ kit) / np.sqrt(HD)
    s_i = (qr @ kit + qi @ krt) / np.sqrt(HD)
    m = np.sqrt(s_r ** 2 + s_i ** 2)
    e = np.exp(m - m.max(-1, keepdims=True))
    eq = mxq(e, 3, "e4m3")
    z = e.sum(-1, keepdims=True)
    o_r = (eq @ mxq(split_heads(v_r), 2, "e4m3")) / z
    o_i = (eq @ mxq(split_heads(v_i), 2, "e4m3")) / z
    return merge_heads(o_r), merge_heads(o_i)

@@ -1,0 +1,330 @@
+from contextlib import ExitStack
+
+import concourse.mybir as mybir
+from concourse.masks import make_identity
+
+F32 = mybir.dt.float32
+BF16 = mybir.dt.bfloat16
+U32 = mybir.dt.uint32
+U8 = mybir.dt.uint8
+FP8X4 = mybir.dt.float8_e4m3fn_x4
+ACT = mybir.ActivationFunctionType
+ALU = mybir.AluOpType
+AXIS = mybir.AxisListType
+
+P = 128
+PACK = 4
+B, S, HD, DX = 8, 512, 128, 1024
+TILES = S // P
+PASSES = DX // (P * PACK)
+BLOCKS = DX // (2 * P)
+REAL, IMAG = 0, 1
+W_R, W_I, W_NEG_I = 0, 1, 2
+WEIGHT_OF = ((W_R, W_I), (W_NEG_I, W_R))
+X_BUFS = 3
+
+FLOPS = 4 * 2 * B * S * DX * HD + 4 * 2 * B * S * S * HD + 2 * 2 * B * S * S * HD
+
+
+def transpose_words(nc, bank, rows, ident_f32):
+    words = rows.bitcast(F32)
+    for i in range(bank.shape[1]):
+        nc.tensor.transpose(bank[:, i, :], words[:, i * P : (i + 1) * P], ident_f32[:])
+
+
+def tile_covenantattention_pa_t_kernel(
+    tc, x_real, x_imag, q_zeta_r, q_zeta_i, k_zeta_r, k_zeta_i, wv_r, wv_i, bv_r, bv_i, out_0, out_1
+):
+    nc = tc.nc
+    x_parts = (x_real, x_imag)
+    outs = (out_0, out_1)
+
+    with ExitStack() as whole:
+        const = whole.enter_context(tc.tile_pool(name="const", bufs=1))
+        m_pool = whole.enter_context(tc.tile_pool(name="m_pool", bufs=1))
+        x_pool = whole.enter_context(tc.tile_pool(name="x_pool", bufs=X_BUFS))
+
+        warm = const.tile([P, 1], F32)
+        nc.vector.memset(warm[:], 1.0)
+        nc.scalar.activation(out=warm[:], in_=warm[:], func=ACT.Sqrt)
+
+        ident_bf = const.tile([P, P], BF16)
+        make_identity(nc, ident_bf[:])
+        ident_f32 = const.tile([P, P], F32)
+        make_identity(nc, ident_f32[:])
+
+        neg_max = const.tile([P, B * TILES], F32)
+        row_sum = const.tile([P, B * TILES], F32)
+        inv_sum = const.tile([P, B * TILES], F32)
+        m_tiles = [m_pool.tile([P, TILES, S], F32, name="m%d" % b) for b in range(B)]
+
+        with ExitStack() as era:
+            nat = era.enter_context(tc.tile_pool(name="nat", bufs=B))
+            flipped = era.enter_context(tc.tile_pool(name="flipped", bufs=2))
+            squares = era.enter_context(tc.tile_pool(name="squares", bufs=3))
+            ps_t = era.enter_context(tc.psum_pool(name="ps_t", bufs=1))
+            ps_s = era.enter_context(tc.psum_pool(name="ps_s", bufs=3))
+
+            qk_nat = []
+            for b in range(B):
+                q_nat = nat.tile([P, 2, TILES, HD], BF16)
+                k_nat = nat.tile([P, 2, TILES, HD], BF16)
+                for part, src in ((REAL, q_zeta_r), (IMAG, q_zeta_i)):
+                    nc.sync.dma_start(
+                        out=q_nat[:, part], in_=src[b, 0].rearrange("(p j) d -> p j d", j=TILES)
+                    )
+                for part, src in ((REAL, k_zeta_r), (IMAG, k_zeta_i)):
+                    nc.sync.dma_start(
+                        out=k_nat[:, part], in_=src[b, 0].rearrange("(p t) d -> p t d", t=TILES)
+                    )
+                qk_nat.append((q_nat, k_nat))
+
+            def flip_qk(b):
+                q_nat, k_nat = qk_nat[b]
+                q_ps = ps_t.tile([P, 2, TILES, P], BF16)
+                k_ps = ps_t.tile([P, 2, TILES, P], BF16)
+                for part in (REAL, IMAG):
+                    for j in range(TILES):
+                        nc.tensor.transpose(q_ps[:, part, j, :], q_nat[:, part, j, :], ident_bf[:])
+                for part in (REAL, IMAG):
+                    for t in range(TILES):
+                        nc.tensor.transpose(k_ps[:, part, t, :], k_nat[:, part, t, :], ident_bf[:])
+                q_t = flipped.tile([P, 2, S], BF16)
+                neg_qi_t = flipped.tile([P, S], BF16)
+                k_t = flipped.tile([P, 2, S], BF16)
+                nc.vector.tensor_copy(
+                    out=q_t[:].rearrange("d c s -> d (c s)"),
+                    in_=q_ps[:].rearrange("d c j p -> d (c j p)"),
+                )
+                nc.vector.tensor_scalar_mul(
+                    out=neg_qi_t[:], in0=q_ps[:, IMAG].rearrange("d j p -> d (j p)"), scalar1=-1.0
+                )
+                nc.vector.tensor_copy(
+                    out=k_t[:].rearrange("d c (u p e) -> d (c u) p e", u=2, e=2),
+                    in_=k_ps[:].rearrange("d c (u e) p -> d (c u) p e", e=2),
+                )
+                return q_t, neg_qi_t, k_t
+
+            def squared_magnitudes(b, q_t, neg_qi_t, k_t):
+                for j in range(TILES):
+                    cols = slice(j * P, (j + 1) * P)
+                    s_r = ps_s.tile([P, S], F32)
+                    s_i = ps_s.tile([P, S], F32)
+                    nc.tensor.matmul(s_r[:], lhsT=q_t[:, REAL, cols], rhs=k_t[:, REAL, :], start=True, stop=False)
+                    nc.tensor.matmul(s_r[:], lhsT=neg_qi_t[:, cols], rhs=k_t[:, IMAG, :], start=False, stop=True)
+                    nc.tensor.matmul(s_i[:], lhsT=q_t[:, REAL, cols], rhs=k_t[:, IMAG, :], start=True, stop=False)
+                    nc.tensor.matmul(s_i[:], lhsT=q_t[:, IMAG, cols], rhs=k_t[:, REAL, :], start=False, stop=True)
+                    sq_r = squares.tile([P, S], F32)
+                    sq_i = squares.tile([P, S], F32)
+                    nc.scalar.activation(out=sq_r[:], in_=s_r[:], func=ACT.Square)
+                    nc.scalar.activation(out=sq_i[:], in_=s_i[:], func=ACT.Square)
+                    nc.vector.tensor_tensor(out=m_tiles[b][:, j, :], in0=sq_r[:], in1=sq_i[:], op=ALU.add)
+
+            def magnitudes(b):
+                flat = m_tiles[b][:].rearrange("p j s -> p (j s)")
+                nc.scalar.activation(out=flat, in_=flat, func=ACT.Sqrt, scale=1.0 / HD)
+
+            def negated_row_max(b):
+                nc.vector.tensor_reduce(
+                    out=neg_max[:, b * TILES : (b + 1) * TILES],
+                    in_=m_tiles[b][:],
+                    axis=AXIS.X,
+                    op=ALU.max,
+                    negate=True,
+                )
+
+            ready = flip_qk(0)
+            for b in range(B):
+                following = flip_qk(b + 1) if b + 1 < B else None
+                squared_magnitudes(b, *ready)
+                ready = following
+                if b >= 1:
+                    magnitudes(b - 1)
+                if b >= 2:
+                    negated_row_max(b - 2)
+            magnitudes(B - 1)
+            negated_row_max(B - 2)
+            negated_row_max(B - 1)
+
+        with ExitStack() as era:
+            w_pool = era.enter_context(tc.tile_pool(name="w_pool", bufs=1, reuse_waits="tile"))
+            stage = era.enter_context(tc.tile_pool(name="stage", bufs=2, reuse_waits="tile"))
+            ps_w = era.enter_context(tc.psum_pool(name="ps_w", bufs=5, reuse_waits="tile"))
+            ps_a = era.enter_context(tc.psum_pool(name="ps_a", bufs=3, reuse_waits="tile"))
+
+            x_nat = {}
+
+            def load_x(b):
+                for part in (REAL, IMAG):
+                    x_sb = x_pool.tile([P, TILES, DX], BF16, name="x_sb%d" % part)
+                    nc.sync.dma_start(
+                        out=x_sb[:], in_=x_parts[part][b].rearrange("(p t) f -> p t f", t=TILES)
+                    )
+                    x_nat[(b, part)] = x_sb
+
+            w_nat = w_pool.tile([P, 3, DX], BF16)
+            nc.sync.dma_start(out=w_nat[:, W_R, :], in_=wv_r)
+            nc.sync.dma_start(out=w_nat[:, W_I, :], in_=wv_i)
+            bias = w_pool.tile([P, 2, HD], BF16)
+            nc.sync.dma_start(out=bias[:, REAL, :], in_=bv_r.partition_broadcast(P))
+            nc.sync.dma_start(out=bias[:, IMAG, :], in_=bv_i.partition_broadcast(P))
+            for b in range(X_BUFS):
+                load_x(b)
+
+            nc.vector.tensor_scalar_mul(out=w_nat[:, W_NEG_I, :], in0=w_nat[:, W_I, :], scalar1=-1.0)
+            w_grouped = w_pool.tile([P, 3, PASSES, HD, PACK], BF16, align_bytes=64)
+            w_codes = w_pool.tile([P, 3, PASSES, HD], U32, align_bytes=64)
+            w_scales = w_pool.tile([P, 3, PASSES, HD], U8, align_bytes=64)
+            for w in range(3):
+                bank = ps_w.tile([P, BLOCKS, P], F32, name="bank", tag="bank")
+                transpose_words(nc, bank, w_nat[:, w, :], ident_f32)
+                nc.vector.tensor_copy(
+                    out=w_grouped[:, w].bitcast(F32),
+                    in_=bank[:].rearrange("p (g u) d -> p g d u", u=2),
+                )
+            for w in range(3):
+                nc.vector.quantize_mx(
+                    out=w_codes[:, w].rearrange("p g d -> p (g d)").bitcast(FP8X4),
+                    scales=w_scales[:, w].rearrange("p g d -> p (g d)"),
+                    in_=w_grouped[:, w].rearrange("p g d j -> p (g d j)"),
+                )
+
+            x_mx = {}
+            e_rows = {}
+            e_mx = {}
+            v_mx = {}
+
+            def quantise_x(b):
+                for part in (REAL, IMAG):
+                    x_sb = x_nat[(b, part)]
+                    x_grouped = stage.tile([P, TILES, PASSES, P, PACK], BF16, align_bytes=64)
+                    for t in range(TILES):
+                        bank = ps_w.tile([P, BLOCKS, P], F32, name="bank", tag="bank")
+                        transpose_words(nc, bank, x_sb[:, t, :], ident_f32)
+                        nc.scalar.copy(
+                            out=x_grouped[:, t].bitcast(F32),
+                            in_=bank[:].rearrange("p (g u) k -> p g k u", u=2),
+                        )
+                    x_codes = stage.tile([P, TILES * PASSES * P], U32, align_bytes=64, name="x_codes%d" % part)
+                    x_scales = stage.tile([P, TILES * PASSES * P], U8, align_bytes=64, name="x_scales%d" % part)
+                    nc.vector.quantize_mx(
+                        out=x_codes[:].bitcast(FP8X4),
+                        scales=x_scales[:],
+                        in_=x_grouped[:].rearrange("p t g k j -> p (t g k j)"),
+                    )
+                    x_mx[(b, part)] = (x_codes, x_scales)
+                if b + X_BUFS < B:
+                    load_x(b + X_BUFS)
+
+            def exponentials(b):
+                e_sb = stage.tile([P, TILES, S], BF16)
+                for j in range(TILES):
+                    col = b * TILES + j
+                    nc.scalar.activation(
+                        out=e_sb[:, j, :],
+                        in_=m_tiles[b][:, j, :],
+                        func=ACT.Exp,
+                        bias=neg_max[:, col : col + 1],
+                        accum_out=row_sum[:, col : col + 1],
+                    )
+                e_rows[b] = e_sb
+
+            def quantise_e(b):
+                e_sb = e_rows[b]
+                e_grouped = stage.tile([P, TILES, P, PACK], BF16, align_bytes=64)
+                for half in range(TILES // 2):
+                    bank = ps_w.tile([P, 2, 2, P], F32, name="bank", tag="bank")
+                    for jj in range(2):
+                        transpose_words(nc, bank[:, jj], e_sb[:, 2 * half + jj, :], ident_f32)
+                    nc.vector.tensor_copy(
+                        out=e_grouped[:, 2 * half : 2 * half + 2].bitcast(F32),
+                        in_=bank[:].rearrange("p j u q -> p j q u"),
+                    )
+                e_codes = stage.tile([P, S], U32, align_bytes=64)
+                e_scales = stage.tile([P, S], U8, align_bytes=64)
+                nc.vector.quantize_mx(
+                    out=e_codes[:].bitcast(FP8X4),
+                    scales=e_scales[:],
+                    in_=e_grouped[:].rearrange("p j q t -> p (j q t)"),
+                )
+                e_mx[b] = (e_codes, e_scales)
+
+            def values(b):
+                v_ps = [ps_a.tile([P, TILES, HD], F32, name="acc", tag="acc") for part in (REAL, IMAG)]
+                steps = [(part, g) for part in (REAL, IMAG) for g in range(PASSES)]
+                for t in range(TILES):
+                    for n, (x_part, g) in enumerate(steps):
+                        x_codes, x_scales = x_mx[(b, x_part)]
+                        cols = slice((t * PASSES + g) * P, (t * PASSES + g + 1) * P)
+                        for v_part in (REAL, IMAG):
+                            w = WEIGHT_OF[x_part][v_part]
+                            nc.tensor.matmul_mx(
+                                out=v_ps[v_part][:, t, :],
+                                lhsT=x_codes[:, cols].bitcast(FP8X4),
+                                lhsT_scale=x_scales[:, cols],
+                                rhs=w_codes[:, w, g, :].bitcast(FP8X4),
+                                rhs_scale=w_scales[:, w, g, :],
+                                start=(n == 0),
+                                stop=(n == len(steps) - 1),
+                            )
+                v_grouped = stage.tile([P, 2, HD, PACK], BF16, align_bytes=64)
+                for v_part in (REAL, IMAG):
+                    nc.vector.tensor_tensor(
+                        out=v_grouped[:, v_part],
+                        in0=v_ps[v_part][:].rearrange("p t d -> p d t"),
+                        in1=bias[:, v_part, :].unsqueeze(2).to_broadcast([P, HD, PACK]),
+                        op=ALU.add,
+                    )
+                v_codes = stage.tile([P, 2 * HD], U32, align_bytes=64)
+                v_scales = stage.tile([P, 2 * HD], U8, align_bytes=64)
+                nc.vector.quantize_mx(
+                    out=v_codes[:].bitcast(FP8X4),
+                    scales=v_scales[:],
+                    in_=v_grouped[:].rearrange("p c d t -> p (c d t)"),
+                )
+                v_mx[b] = (v_codes, v_scales)
+
+            def outputs(b):
+                e_codes, e_scales = e_mx[b]
+                v_codes, v_scales = v_mx[b]
+                cols_b = slice(b * TILES, (b + 1) * TILES)
+                nc.vector.reciprocal(out=inv_sum[:, cols_b], in_=row_sum[:, cols_b])
+                o_sb = stage.tile([P, 2, TILES, HD], F32)
+                for half in range(TILES // 2):
+                    o_ps = ps_a.tile([P, 2, 2 * HD], F32, name="acc", tag="acc")
+                    for jj in range(2):
+                        j = 2 * half + jj
+                        cols = slice(j * P, (j + 1) * P)
+                        nc.tensor.matmul_mx(
+                            out=o_ps[:, jj, :],
+                            lhsT=e_codes[:, cols].bitcast(FP8X4),
+                            lhsT_scale=e_scales[:, cols],
+                            rhs=v_codes[:].bitcast(FP8X4),
+                            rhs_scale=v_scales[:],
+                            start=True,
+                            stop=True,
+                        )
+                    for jj in range(2):
+                        j = 2 * half + jj
+                        col = b * TILES + j
+                        nc.vector.tensor_scalar_mul(
+                            out=o_sb[:, :, j, :],
+                            in0=o_ps[:, jj, :].rearrange("p (c d) -> p c d", c=2),
+                            scalar1=inv_sum[:, col : col + 1],
+                        )
+                for part in (REAL, IMAG):
+                    nc.sync.dma_start(
+                        out=outs[part][b].rearrange("(p j) d -> p j d", j=TILES), in_=o_sb[:, part]
+                    )
+
+            exponentials(0)
+            quantise_x(0)
+            for b in range(B):
+                quantise_e(b)
+                if b + 1 < B:
+                    quantise_x(b + 1)
+                    exponentials(b + 1)
+                values(b)
+                if b >= 1:
+                    outputs(b - 1)
+            outputs(B - 1)

@@ -40,9 +40,11 @@ def tile_covenantattention_pa_t_kernel(
     outs = (out_0, out_1)
 
     with ExitStack() as whole:
+        whole.enter_context(tc.manual_schedule())
         const = whole.enter_context(tc.tile_pool(name="const", bufs=1))
         m_pool = whole.enter_context(tc.tile_pool(name="m_pool", bufs=1))
         x_pool = whole.enter_context(tc.tile_pool(name="x_pool", bufs=X_BUFS))
+        psum = whole.enter_context(tc.psum_pool(name="psum", bufs=8))
 
         warm = const.tile([P, 1], F32)
         nc.vector.memset(warm[:], 1.0)
@@ -58,12 +60,51 @@ def tile_covenantattention_pa_t_kernel(
         inv_sum = const.tile([P, B * TILES], F32)
         m_tiles = [m_pool.tile([P, TILES, S], F32, name="m%d" % b) for b in range(B)]
 
+        w_nat = const.tile([P, 3, DX], BF16)
+        bias = const.tile([P, 2, HD], BF16)
+        w_grouped = const.tile([P, 3, PASSES, HD, PACK], BF16, align_bytes=64)
+        w_codes = const.tile([P, 3, PASSES, HD], U32, align_bytes=64)
+        w_scales = const.tile([P, 3, PASSES, HD], U8, align_bytes=64)
+        x_nat = {}
+
+        def load_x(b):
+            for part in (REAL, IMAG):
+                x_sb = x_pool.tile([P, TILES, DX], BF16, name="x_sb%d" % part, tag="x_sb%d" % part)
+                nc.sync.dma_start(
+                    out=x_sb[:], in_=x_parts[part][b].rearrange("(p t) f -> p t f", t=TILES)
+                )
+                x_nat[(b, part)] = x_sb
+
+        def quantise_weights():
+            nc.vector.tensor_scalar_mul(out=w_nat[:, W_NEG_I, :], in0=w_nat[:, W_I, :], scalar1=-1.0)
+            for w in range(3):
+                bank = psum.tile([P, BLOCKS, P], F32, name="bank", tag="bank")
+                transpose_words(nc, bank, w_nat[:, w, :], ident_f32)
+                nc.vector.tensor_copy(
+                    out=w_grouped[:, w].bitcast(F32),
+                    in_=bank[:].rearrange("p (g u) d -> p g d u", u=2),
+                )
+            for w in range(3):
+                nc.vector.quantize_mx(
+                    out=w_codes[:, w].rearrange("p g d -> p (g d)").bitcast(FP8X4),
+                    scales=w_scales[:, w].rearrange("p g d -> p (g d)"),
+                    in_=w_grouped[:, w].rearrange("p g d j -> p (g d j)"),
+                )
+
+        def magnitudes(b):
+            flat = m_tiles[b][:].rearrange("p j s -> p (j s)")
+            nc.scalar.activation(out=flat, in_=flat, func=ACT.Sqrt, scale=1.0 / HD)
+
+        def negated_row_max(b, j):
+            col = b * TILES + j
+            nc.vector.tensor_reduce(
+                out=neg_max[:, col : col + 1], in_=m_tiles[b][:, j, :], axis=AXIS.X, op=ALU.max, negate=True
+            )
+
         with ExitStack() as era:
             nat = era.enter_context(tc.tile_pool(name="nat", bufs=B))
-            flipped = era.enter_context(tc.tile_pool(name="flipped", bufs=2))
+            flipped = era.enter_context(tc.tile_pool(name="flipped", bufs=3))
             squares = era.enter_context(tc.tile_pool(name="squares", bufs=3))
-            ps_t = era.enter_context(tc.psum_pool(name="ps_t", bufs=1))
-            ps_s = era.enter_context(tc.psum_pool(name="ps_s", bufs=3))
 
             qk_nat = []
             for b in range(B):
@@ -78,11 +119,19 @@ def tile_covenantattention_pa_t_kernel(
                         out=k_nat[:, part], in_=src[b, 0].rearrange("(p t) d -> p t d", t=TILES)
                     )
                 qk_nat.append((q_nat, k_nat))
+            nc.sync.dma_start(out=w_nat[:, W_R, :], in_=wv_r)
+            nc.sync.dma_start(out=w_nat[:, W_I, :], in_=wv_i)
+            nc.sync.dma_start(out=bias[:, REAL, :], in_=bv_r.partition_broadcast(P))
+            nc.sync.dma_start(out=bias[:, IMAG, :], in_=bv_i.partition_broadcast(P))
+            for b in range(X_BUFS):
+                load_x(b)
+
+            qk_t = {}
 
             def flip_qk(b):
                 q_nat, k_nat = qk_nat[b]
-                q_ps = ps_t.tile([P, 2, TILES, P], BF16)
-                k_ps = ps_t.tile([P, 2, TILES, P], BF16)
+                q_ps = psum.tile([P, 2, TILES, P], BF16, name="bank", tag="bank")
+                k_ps = psum.tile([P, 2, TILES, P], BF16, name="bank", tag="bank")
                 for part in (REAL, IMAG):
                     for j in range(TILES):
                         nc.tensor.transpose(q_ps[:, part, j, :], q_nat[:, part, j, :], ident_bf[:])
@@ -103,118 +152,76 @@ def tile_covenantattention_pa_t_kernel(
                     out=k_t[:].rearrange("d c (u p e) -> d (c u) p e", u=2, e=2),
                     in_=k_ps[:].rearrange("d c (u e) p -> d (c u) p e", e=2),
                 )
-                return q_t, neg_qi_t, k_t
+                qk_t[b] = (q_t, neg_qi_t, k_t)
 
-            def squared_magnitudes(b, q_t, neg_qi_t, k_t):
-                for j in range(TILES):
-                    cols = slice(j * P, (j + 1) * P)
-                    s_r = ps_s.tile([P, S], F32)
-                    s_i = ps_s.tile([P, S], F32)
-                    nc.tensor.matmul(s_r[:], lhsT=q_t[:, REAL, cols], rhs=k_t[:, REAL, :], start=True, stop=False)
-                    nc.tensor.matmul(s_r[:], lhsT=neg_qi_t[:, cols], rhs=k_t[:, IMAG, :], start=False, stop=True)
-                    nc.tensor.matmul(s_i[:], lhsT=q_t[:, REAL, cols], rhs=k_t[:, IMAG, :], start=True, stop=False)
-                    nc.tensor.matmul(s_i[:], lhsT=q_t[:, IMAG, cols], rhs=k_t[:, REAL, :], start=False, stop=True)
-                    sq_r = squares.tile([P, S], F32)
-                    sq_i = squares.tile([P, S], F32)
-                    nc.scalar.activation(out=sq_r[:], in_=s_r[:], func=ACT.Square)
-                    nc.scalar.activation(out=sq_i[:], in_=s_i[:], func=ACT.Square)
-                    nc.vector.tensor_tensor(out=m_tiles[b][:, j, :], in0=sq_r[:], in1=sq_i[:], op=ALU.add)
+            def squared_magnitudes(b, j):
+                q_t, neg_qi_t, k_t = qk_t[b]
+                cols = slice(j * P, (j + 1) * P)
+                s_r = psum.tile([P, S], F32, name="bank", tag="bank")
+                s_i = psum.tile([P, S], F32, name="bank", tag="bank")
+                nc.tensor.matmul(s_r[:], lhsT=q_t[:, REAL, cols], rhs=k_t[:, REAL, :], start=True, stop=False)
+                nc.tensor.matmul(s_r[:], lhsT=neg_qi_t[:, cols], rhs=k_t[:, IMAG, :], start=False, stop=True)
+                nc.tensor.matmul(s_i[:], lhsT=q_t[:, REAL, cols], rhs=k_t[:, IMAG, :], start=True, stop=False)
+                nc.tensor.matmul(s_i[:], lhsT=q_t[:, IMAG, cols], rhs=k_t[:, REAL, :], start=False, stop=True)
+                sq_r = squares.tile([P, S], F32)
+                sq_i = squares.tile([P, S], F32)
+                nc.scalar.activation(out=sq_r[:], in_=s_r[:], func=ACT.Square)
+                nc.scalar.activation(out=sq_i[:], in_=s_i[:], func=ACT.Square)
+                nc.vector.tensor_tensor(out=m_tiles[b][:, j, :], in0=sq_r[:], in1=sq_i[:], op=ALU.add)
 
-            def magnitudes(b):
-                flat = m_tiles[b][:].rearrange("p j s -> p (j s)")
-                nc.scalar.activation(out=flat, in_=flat, func=ACT.Sqrt, scale=1.0 / HD)
-
-            def negated_row_max(b):
-                nc.vector.tensor_reduce(
-                    out=neg_max[:, b * TILES : (b + 1) * TILES],
-                    in_=m_tiles[b][:],
-                    axis=AXIS.X,
-                    op=ALU.max,
-                    negate=True,
-                )
-
-            ready = flip_qk(0)
+            flip_qk(0)
+            flip_qk(1)
             for b in range(B):
-                following = flip_qk(b + 1) if b + 1 < B else None
-                squared_magnitudes(b, *ready)
-                ready = following
+                for j in range(TILES):
+                    squared_magnitudes(b, j)
+                    if b >= 2:
+                        negated_row_max(b - 2, j)
+                if b + 2 < B:
+                    flip_qk(b + 2)
+                if b + 2 == B:
+                    quantise_weights()
                 if b >= 1:
                     magnitudes(b - 1)
-                if b >= 2:
-                    negated_row_max(b - 2)
             magnitudes(B - 1)
-            negated_row_max(B - 2)
-            negated_row_max(B - 1)
+            for j in range(TILES):
+                negated_row_max(B - 2, j)
 
         with ExitStack() as era:
-            w_pool = era.enter_context(tc.tile_pool(name="w_pool", bufs=1, reuse_waits="tile"))
             stage = era.enter_context(tc.tile_pool(name="stage", bufs=2, reuse_waits="tile"))
-            ps_w = era.enter_context(tc.psum_pool(name="ps_w", bufs=5, reuse_waits="tile"))
-            ps_a = era.enter_context(tc.psum_pool(name="ps_a", bufs=3, reuse_waits="tile"))
 
-            x_nat = {}
-
-            def load_x(b):
-                for part in (REAL, IMAG):
-                    x_sb = x_pool.tile([P, TILES, DX], BF16, name="x_sb%d" % part)
-                    nc.sync.dma_start(
-                        out=x_sb[:], in_=x_parts[part][b].rearrange("(p t) f -> p t f", t=TILES)
-                    )
-                    x_nat[(b, part)] = x_sb
-
-            w_nat = w_pool.tile([P, 3, DX], BF16)
-            nc.sync.dma_start(out=w_nat[:, W_R, :], in_=wv_r)
-            nc.sync.dma_start(out=w_nat[:, W_I, :], in_=wv_i)
-            bias = w_pool.tile([P, 2, HD], BF16)
-            nc.sync.dma_start(out=bias[:, REAL, :], in_=bv_r.partition_broadcast(P))
-            nc.sync.dma_start(out=bias[:, IMAG, :], in_=bv_i.partition_broadcast(P))
-            for b in range(X_BUFS):
-                load_x(b)
-
-            nc.vector.tensor_scalar_mul(out=w_nat[:, W_NEG_I, :], in0=w_nat[:, W_I, :], scalar1=-1.0)
-            w_grouped = w_pool.tile([P, 3, PASSES, HD, PACK], BF16, align_bytes=64)
-            w_codes = w_pool.tile([P, 3, PASSES, HD], U32, align_bytes=64)
-            w_scales = w_pool.tile([P, 3, PASSES, HD], U8, align_bytes=64)
-            for w in range(3):
-                bank = ps_w.tile([P, BLOCKS, P], F32, name="bank", tag="bank")
-                transpose_words(nc, bank, w_nat[:, w, :], ident_f32)
-                nc.vector.tensor_copy(
-                    out=w_grouped[:, w].bitcast(F32),
-                    in_=bank[:].rearrange("p (g u) d -> p g d u", u=2),
-                )
-            for w in range(3):
-                nc.vector.quantize_mx(
-                    out=w_codes[:, w].rearrange("p g d -> p (g d)").bitcast(FP8X4),
-                    scales=w_scales[:, w].rearrange("p g d -> p (g d)"),
-                    in_=w_grouped[:, w].rearrange("p g d j -> p (g d j)"),
-                )
-
+            x_words = {}
             x_mx = {}
             e_rows = {}
+            e_words = {}
             e_mx = {}
+            v_words = {}
             v_mx = {}
 
-            def quantise_x(b):
-                for part in (REAL, IMAG):
-                    x_sb = x_nat[(b, part)]
-                    x_grouped = stage.tile([P, TILES, PASSES, P, PACK], BF16, align_bytes=64)
-                    for t in range(TILES):
-                        bank = ps_w.tile([P, BLOCKS, P], F32, name="bank", tag="bank")
-                        transpose_words(nc, bank, x_sb[:, t, :], ident_f32)
-                        nc.scalar.copy(
-                            out=x_grouped[:, t].bitcast(F32),
-                            in_=bank[:].rearrange("p (g u) k -> p g k u", u=2),
-                        )
-                    x_codes = stage.tile([P, TILES * PASSES * P], U32, align_bytes=64, name="x_codes%d" % part)
-                    x_scales = stage.tile([P, TILES * PASSES * P], U8, align_bytes=64, name="x_scales%d" % part)
-                    nc.vector.quantize_mx(
-                        out=x_codes[:].bitcast(FP8X4),
-                        scales=x_scales[:],
-                        in_=x_grouped[:].rearrange("p t g k j -> p (t g k j)"),
+            def flip_x(b, part):
+                x_sb = x_nat[(b, part)]
+                x_grouped = stage.tile([P, TILES, PASSES, P, PACK], BF16, align_bytes=64)
+                for t in range(TILES):
+                    bank = psum.tile([P, BLOCKS, P], F32, name="bank", tag="bank")
+                    transpose_words(nc, bank, x_sb[:, t, :], ident_f32)
+                    nc.scalar.copy(
+                        out=x_grouped[:, t].bitcast(F32),
+                        in_=bank[:].rearrange("p (g u) k -> p g k u", u=2),
                     )
-                    x_mx[(b, part)] = (x_codes, x_scales)
-                if b + X_BUFS < B:
-                    load_x(b + X_BUFS)
+                x_words[(b, part)] = x_grouped
+
+            def quantise_x(b, part):
+                x_codes = stage.tile(
+                    [P, TILES * PASSES * P], U32, align_bytes=64, name="x_codes%d" % part, tag="x_codes%d" % part
+                )
+                x_scales = stage.tile(
+                    [P, TILES * PASSES * P], U8, align_bytes=64, name="x_scales%d" % part, tag="x_scales%d" % part
+                )
+                nc.vector.quantize_mx(
+                    out=x_codes[:].bitcast(FP8X4),
+                    scales=x_scales[:],
+                    in_=x_words[(b, part)][:].rearrange("p t g k j -> p (t g k j)"),
+                )
+                x_mx[(b, part)] = (x_codes, x_scales)
 
             def exponentials(b):
                 e_sb = stage.tile([P, TILES, S], BF16)
@@ -229,28 +236,31 @@ def tile_covenantattention_pa_t_kernel(
                     )
                 e_rows[b] = e_sb
 
-            def quantise_e(b):
+            def flip_e(b):
                 e_sb = e_rows[b]
                 e_grouped = stage.tile([P, TILES, P, PACK], BF16, align_bytes=64)
                 for half in range(TILES // 2):
-                    bank = ps_w.tile([P, 2, 2, P], F32, name="bank", tag="bank")
+                    bank = psum.tile([P, 2, 2, P], F32, name="bank", tag="bank")
                     for jj in range(2):
                         transpose_words(nc, bank[:, jj], e_sb[:, 2 * half + jj, :], ident_f32)
                     nc.vector.tensor_copy(
                         out=e_grouped[:, 2 * half : 2 * half + 2].bitcast(F32),
                         in_=bank[:].rearrange("p j u q -> p j q u"),
                     )
+                e_words[b] = e_grouped
+
+            def quantise_e(b):
                 e_codes = stage.tile([P, S], U32, align_bytes=64)
                 e_scales = stage.tile([P, S], U8, align_bytes=64)
                 nc.vector.quantize_mx(
                     out=e_codes[:].bitcast(FP8X4),
                     scales=e_scales[:],
-                    in_=e_grouped[:].rearrange("p j q t -> p (j q t)"),
+                    in_=e_words[b][:].rearrange("p j q t -> p (j q t)"),
                 )
                 e_mx[b] = (e_codes, e_scales)
 
             def values(b):
-                v_ps = [ps_a.tile([P, TILES, HD], F32, name="acc", tag="acc") for part in (REAL, IMAG)]
+                v_ps = [psum.tile([P, TILES, HD], F32, name="bank", tag="bank") for part in (REAL, IMAG)]
                 steps = [(part, g) for part in (REAL, IMAG) for g in range(PASSES)]
                 for t in range(TILES):
                     for n, (x_part, g) in enumerate(steps):
@@ -275,12 +285,15 @@ def tile_covenantattention_pa_t_kernel(
                         in1=bias[:, v_part, :].unsqueeze(2).to_broadcast([P, HD, PACK]),
                         op=ALU.add,
                     )
+                v_words[b] = v_grouped
+
+            def quantise_v(b):
                 v_codes = stage.tile([P, 2 * HD], U32, align_bytes=64)
                 v_scales = stage.tile([P, 2 * HD], U8, align_bytes=64)
                 nc.vector.quantize_mx(
                     out=v_codes[:].bitcast(FP8X4),
                     scales=v_scales[:],
-                    in_=v_grouped[:].rearrange("p c d t -> p (c d t)"),
+                    in_=v_words[b][:].rearrange("p c d t -> p (c d t)"),
                 )
                 v_mx[b] = (v_codes, v_scales)
 
@@ -291,7 +304,7 @@ def tile_covenantattention_pa_t_kernel(
                 nc.vector.reciprocal(out=inv_sum[:, cols_b], in_=row_sum[:, cols_b])
                 o_sb = stage.tile([P, 2, TILES, HD], F32)
                 for half in range(TILES // 2):
-                    o_ps = ps_a.tile([P, 2, 2 * HD], F32, name="acc", tag="acc")
+                    o_ps = psum.tile([P, 2, 2 * HD], F32, name="bank", tag="bank")
                     for jj in range(2):
                         j = 2 * half + jj
                         cols = slice(j * P, (j + 1) * P)
@@ -317,14 +330,30 @@ def tile_covenantattention_pa_t_kernel(
                         out=outs[part][b].rearrange("(p j) d -> p j d", j=TILES), in_=o_sb[:, part]
                     )
 
+            flip_x(0, REAL)
+            for j in range(TILES):
+                negated_row_max(B - 1, j)
+            quantise_x(0, REAL)
+            flip_x(0, IMAG)
+            quantise_x(0, IMAG)
+            load_x(X_BUFS)
             exponentials(0)
-            quantise_x(0)
             for b in range(B):
+                ahead = b + 1
+                if ahead < B:
+                    flip_x(ahead, REAL)
+                flip_e(b)
+                if ahead < B:
+                    quantise_x(ahead, REAL)
                 quantise_e(b)
-                if b + 1 < B:
-                    quantise_x(b + 1)
-                    exponentials(b + 1)
+                if ahead < B:
+                    flip_x(ahead, IMAG)
+                    quantise_x(ahead, IMAG)
+                    if ahead + X_BUFS < B:
+                        load_x(ahead + X_BUFS)
+                    exponentials(ahead)
                 values(b)
                 if b >= 1:
                     outputs(b - 1)
+                quantise_v(b)
             outputs(B - 1)

@@ -21,7 +21,8 @@ BLOCKS = DX // (2 * P)
 REAL, IMAG = 0, 1
 W_R, W_I, W_NEG_I = 0, 1, 2
 WEIGHT_OF = ((W_R, W_I), (W_NEG_I, W_R))
-X_BUFS = 3
+X_BUFS = 2
+QK_BUFS = 4
 
 FLOPS = 4 * 2 * B * S * DX * HD + 4 * 2 * B * S * S * HD + 2 * 2 * B * S * S * HD
 
@@ -43,7 +44,6 @@ def tile_covenantattention_pa_t_kernel(
         whole.enter_context(tc.manual_schedule())
         const = whole.enter_context(tc.tile_pool(name="const", bufs=1))
         m_pool = whole.enter_context(tc.tile_pool(name="m_pool", bufs=1))
-        x_pool = whole.enter_context(tc.tile_pool(name="x_pool", bufs=X_BUFS))
         psum = whole.enter_context(tc.psum_pool(name="psum", bufs=8))
 
         warm = const.tile([P, 1], F32)
@@ -65,31 +65,8 @@ def tile_covenantattention_pa_t_kernel(
         w_grouped = const.tile([P, 3, PASSES, HD, PACK], BF16, align_bytes=64)
         w_codes = const.tile([P, 3, PASSES, HD], U32, align_bytes=64)
         w_scales = const.tile([P, 3, PASSES, HD], U8, align_bytes=64)
-        x_nat = {}
-
-        def load_x(b):
-            for part in (REAL, IMAG):
-                x_sb = x_pool.tile([P, TILES, DX], BF16, name="x_sb%d" % part, tag="x_sb%d" % part)
-                nc.sync.dma_start(
-                    out=x_sb[:], in_=x_parts[part][b].rearrange("(p t) f -> p t f", t=TILES)
-                )
-                x_nat[(b, part)] = x_sb
-
-        def quantise_weights():
-            nc.vector.tensor_scalar_mul(out=w_nat[:, W_NEG_I, :], in0=w_nat[:, W_I, :], scalar1=-1.0)
-            for w in range(3):
-                bank = psum.tile([P, BLOCKS, P], F32, name="bank", tag="bank")
-                transpose_words(nc, bank, w_nat[:, w, :], ident_f32)
-                nc.vector.tensor_copy(
-                    out=w_grouped[:, w].bitcast(F32),
-                    in_=bank[:].rearrange("p (g u) d -> p g d u", u=2),
-                )
-            for w in range(3):
-                nc.vector.quantize_mx(
-                    out=w_codes[:, w].rearrange("p g d -> p (g d)").bitcast(FP8X4),
-                    scales=w_scales[:, w].rearrange("p g d -> p (g d)"),
-                    in_=w_grouped[:, w].rearrange("p g d j -> p (g d j)"),
-                )
+        v_codes = const.tile([P, B, 2 * HD], U32, align_bytes=64)
+        v_scales = const.tile([P, B, 2 * HD], U8, align_bytes=64)
 
         def magnitudes(b):
             flat = m_tiles[b][:].rearrange("p j s -> p (j s)")
@@ -101,13 +78,30 @@ def tile_covenantattention_pa_t_kernel(
                 out=neg_max[:, col : col + 1], in_=m_tiles[b][:, j, :], axis=AXIS.X, op=ALU.max, negate=True
             )
 
-        with ExitStack() as era:
-            nat = era.enter_context(tc.tile_pool(name="nat", bufs=B))
-            flipped = era.enter_context(tc.tile_pool(name="flipped", bufs=3))
-            squares = era.enter_context(tc.tile_pool(name="squares", bufs=3))
+        with ExitStack() as phase:
+            x_pool = phase.enter_context(tc.tile_pool(name="x_pool", bufs=X_BUFS))
+            nat = phase.enter_context(tc.tile_pool(name="nat", bufs=QK_BUFS))
+            flipped = phase.enter_context(tc.tile_pool(name="flipped", bufs=2))
+            squares = phase.enter_context(tc.tile_pool(name="squares", bufs=3))
+            x_stage = phase.enter_context(tc.tile_pool(name="x_stage", bufs=3))
+            x_keep = phase.enter_context(tc.tile_pool(name="x_keep", bufs=2))
 
-            qk_nat = []
-            for b in range(B):
+            x_nat = {}
+            qk_nat = {}
+            qk_t = {}
+            x_words = {}
+            x_mx = {}
+            v_words = {}
+
+            def load_x(b):
+                for part in (REAL, IMAG):
+                    x_sb = x_pool.tile([P, TILES, DX], BF16, name="x_sb%d" % part, tag="x_sb%d" % part)
+                    nc.sync.dma_start(
+                        out=x_sb[:], in_=x_parts[part][b].rearrange("(p t) f -> p t f", t=TILES)
+                    )
+                    x_nat[(b, part)] = x_sb
+
+            def load_qk(b):
                 q_nat = nat.tile([P, 2, TILES, HD], BF16)
                 k_nat = nat.tile([P, 2, TILES, HD], BF16)
                 for part, src in ((REAL, q_zeta_r), (IMAG, q_zeta_i)):
@@ -118,15 +112,23 @@ def tile_covenantattention_pa_t_kernel(
                     nc.sync.dma_start(
                         out=k_nat[:, part], in_=src[b, 0].rearrange("(p t) d -> p t d", t=TILES)
                     )
-                qk_nat.append((q_nat, k_nat))
-            nc.sync.dma_start(out=w_nat[:, W_R, :], in_=wv_r)
-            nc.sync.dma_start(out=w_nat[:, W_I, :], in_=wv_i)
-            nc.sync.dma_start(out=bias[:, REAL, :], in_=bv_r.partition_broadcast(P))
-            nc.sync.dma_start(out=bias[:, IMAG, :], in_=bv_i.partition_broadcast(P))
-            for b in range(X_BUFS):
-                load_x(b)
+                qk_nat[b] = (q_nat, k_nat)
 
-            qk_t = {}
+            def quantise_weights():
+                nc.vector.tensor_scalar_mul(out=w_nat[:, W_NEG_I, :], in0=w_nat[:, W_I, :], scalar1=-1.0)
+                for w in range(3):
+                    bank = psum.tile([P, BLOCKS, P], F32, name="bank", tag="bank")
+                    transpose_words(nc, bank, w_nat[:, w, :], ident_f32)
+                    nc.vector.tensor_copy(
+                        out=w_grouped[:, w].bitcast(F32),
+                        in_=bank[:].rearrange("p (g u) d -> p g d u", u=2),
+                    )
+                for w in range(3):
+                    nc.vector.quantize_mx(
+                        out=w_codes[:, w].rearrange("p g d -> p (g d)").bitcast(FP8X4),
+                        scales=w_scales[:, w].rearrange("p g d -> p (g d)"),
+                        in_=w_grouped[:, w].rearrange("p g d j -> p (g d j)"),
+                    )
 
             def flip_qk(b):
                 q_nat, k_nat = qk_nat[b]
@@ -153,78 +155,140 @@ def tile_covenantattention_pa_t_kernel(
                     in_=k_ps[:].rearrange("d c (u e) p -> d (c u) p e", e=2),
                 )
                 qk_t[b] = (q_t, neg_qi_t, k_t)
+                if b + QK_BUFS < B:
+                    load_qk(b + QK_BUFS)
 
-            def squared_magnitudes(b, j):
+            def scores_and_x(b, j):
                 q_t, neg_qi_t, k_t = qk_t[b]
                 cols = slice(j * P, (j + 1) * P)
                 s_r = psum.tile([P, S], F32, name="bank", tag="bank")
+                x_r = psum.tile([P, BLOCKS, P], F32, name="bank", tag="bank")
                 s_i = psum.tile([P, S], F32, name="bank", tag="bank")
-                nc.tensor.matmul(s_r[:], lhsT=q_t[:, REAL, cols], rhs=k_t[:, REAL, :], start=True, stop=False)
-                nc.tensor.matmul(s_r[:], lhsT=neg_qi_t[:, cols], rhs=k_t[:, IMAG, :], start=False, stop=True)
-                nc.tensor.matmul(s_i[:], lhsT=q_t[:, REAL, cols], rhs=k_t[:, IMAG, :], start=True, stop=False)
-                nc.tensor.matmul(s_i[:], lhsT=q_t[:, IMAG, cols], rhs=k_t[:, REAL, :], start=False, stop=True)
+                x_i = psum.tile([P, BLOCKS, P], F32, name="bank", tag="bank")
+                products = (
+                    (s_r, q_t[:, REAL, cols], REAL, x_r),
+                    (s_r, neg_qi_t[:, cols], IMAG, x_r),
+                    (s_i, q_t[:, REAL, cols], IMAG, x_i),
+                    (s_i, q_t[:, IMAG, cols], REAL, x_i),
+                )
+                for n, (acc, q_cols, k_part, x_bank) in enumerate(products):
+                    second = n % 2
+                    nc.tensor.matmul(
+                        acc[:], lhsT=q_cols, rhs=k_t[:, k_part, :], start=(second == 0), stop=(second == 1)
+                    )
+                    words = x_nat[(b, n // 2)][:, j, :].bitcast(F32)
+                    for i in (2 * second, 2 * second + 1):
+                        nc.tensor.transpose(x_bank[:, i, :], words[:, i * P : (i + 1) * P], ident_f32[:])
                 sq_r = squares.tile([P, S], F32)
                 sq_i = squares.tile([P, S], F32)
+                x_grouped = x_stage.tile([P, 2, PASSES, P, PACK], BF16, align_bytes=64)
                 nc.scalar.activation(out=sq_r[:], in_=s_r[:], func=ACT.Square)
+                nc.scalar.copy(
+                    out=x_grouped[:, REAL].bitcast(F32), in_=x_r[:].rearrange("p (g u) k -> p g k u", u=2)
+                )
                 nc.scalar.activation(out=sq_i[:], in_=s_i[:], func=ACT.Square)
+                nc.scalar.copy(
+                    out=x_grouped[:, IMAG].bitcast(F32), in_=x_i[:].rearrange("p (g u) k -> p g k u", u=2)
+                )
                 nc.vector.tensor_tensor(out=m_tiles[b][:, j, :], in0=sq_r[:], in1=sq_i[:], op=ALU.add)
+                x_words[(b, j)] = x_grouped
+
+            def quantise_x(b, j):
+                if j == 0:
+                    x_codes = x_keep.tile([P, TILES, 2, PASSES, P], U32, align_bytes=64)
+                    x_scales = x_keep.tile([P, TILES, 2, PASSES, P], U8, align_bytes=64)
+                    x_mx[b] = (x_codes, x_scales)
+                x_codes, x_scales = x_mx[b]
+                nc.vector.quantize_mx(
+                    out=x_codes[:, j].rearrange("p c g k -> p (c g k)").bitcast(FP8X4),
+                    scales=x_scales[:, j].rearrange("p c g k -> p (c g k)"),
+                    in_=x_words[(b, j)][:].rearrange("p c g k t -> p (c g k t)"),
+                )
+
+            def values(b):
+                x_codes, x_scales = x_mx[b]
+                v_ps = [psum.tile([P, TILES, HD], F32, name="bank", tag="bank") for part in (REAL, IMAG)]
+                steps = [(part, g) for part in (REAL, IMAG) for g in range(PASSES)]
+                for t in range(TILES):
+                    for n, (x_part, g) in enumerate(steps):
+                        for v_part in (REAL, IMAG):
+                            w = WEIGHT_OF[x_part][v_part]
+                            nc.tensor.matmul_mx(
+                                out=v_ps[v_part][:, t, :],
+                                lhsT=x_codes[:, t, x_part, g, :].bitcast(FP8X4),
+                                lhsT_scale=x_scales[:, t, x_part, g, :],
+                                rhs=w_codes[:, w, g, :].bitcast(FP8X4),
+                                rhs_scale=w_scales[:, w, g, :],
+                                start=(n == 0),
+                                stop=(n == len(steps) - 1),
+                            )
+                v_grouped = x_stage.tile([P, 2, HD, PACK], BF16, align_bytes=64)
+                for v_part in (REAL, IMAG):
+                    nc.vector.tensor_tensor(
+                        out=v_grouped[:, v_part],
+                        in0=v_ps[v_part][:].rearrange("p t d -> p d t"),
+                        in1=bias[:, v_part, :].unsqueeze(2).to_broadcast([P, HD, PACK]),
+                        op=ALU.add,
+                    )
+                v_words[b] = v_grouped
+
+            def quantise_v(b):
+                nc.vector.quantize_mx(
+                    out=v_codes[:, b, :].bitcast(FP8X4),
+                    scales=v_scales[:, b, :],
+                    in_=v_words[b][:].rearrange("p c d t -> p (c d t)"),
+                )
+
+            load_qk(0)
+            load_x(0)
+            load_qk(1)
+            nc.sync.dma_start(out=w_nat[:, W_R, :], in_=wv_r)
+            nc.sync.dma_start(out=w_nat[:, W_I, :], in_=wv_i)
+            load_x(1)
+            for b in range(2, QK_BUFS):
+                load_qk(b)
+            nc.sync.dma_start(out=bias[:, REAL, :], in_=bv_r.partition_broadcast(P))
+            nc.sync.dma_start(out=bias[:, IMAG, :], in_=bv_i.partition_broadcast(P))
 
             flip_qk(0)
-            flip_qk(1)
             for b in range(B):
                 for j in range(TILES):
-                    squared_magnitudes(b, j)
+                    scores_and_x(b, j)
                     if b >= 2:
                         negated_row_max(b - 2, j)
-                if b + 2 < B:
-                    flip_qk(b + 2)
-                if b + 2 == B:
+                    if j >= 1:
+                        quantise_x(b, j - 1)
+                    if b >= 1 and j == 1:
+                        values(b - 1)
+                    if b + 1 < B and j == 2:
+                        flip_qk(b + 1)
+                    if b >= 1 and j == 3:
+                        quantise_v(b - 1)
+                quantise_x(b, TILES - 1)
+                if b + X_BUFS < B:
+                    load_x(b + X_BUFS)
+                if b == 0:
                     quantise_weights()
                 if b >= 1:
                     magnitudes(b - 1)
             magnitudes(B - 1)
+            values(B - 1)
             for j in range(TILES):
                 negated_row_max(B - 2, j)
+            quantise_v(B - 1)
+            for j in range(TILES):
+                negated_row_max(B - 1, j)
 
-        with ExitStack() as era:
-            stage = era.enter_context(tc.tile_pool(name="stage", bufs=2, reuse_waits="tile"))
+        with ExitStack() as phase:
+            stage = phase.enter_context(tc.tile_pool(name="stage", bufs=2, reuse_waits="tile"))
+            e_pool = phase.enter_context(tc.tile_pool(name="e_pool", bufs=3, reuse_waits="tile"))
 
-            x_words = {}
-            x_mx = {}
             e_rows = {}
             e_words = {}
             e_mx = {}
-            v_words = {}
-            v_mx = {}
-
-            def flip_x(b, part):
-                x_sb = x_nat[(b, part)]
-                x_grouped = stage.tile([P, TILES, PASSES, P, PACK], BF16, align_bytes=64)
-                for t in range(TILES):
-                    bank = psum.tile([P, BLOCKS, P], F32, name="bank", tag="bank")
-                    transpose_words(nc, bank, x_sb[:, t, :], ident_f32)
-                    nc.scalar.copy(
-                        out=x_grouped[:, t].bitcast(F32),
-                        in_=bank[:].rearrange("p (g u) k -> p g k u", u=2),
-                    )
-                x_words[(b, part)] = x_grouped
-
-            def quantise_x(b, part):
-                x_codes = stage.tile(
-                    [P, TILES * PASSES * P], U32, align_bytes=64, name="x_codes%d" % part, tag="x_codes%d" % part
-                )
-                x_scales = stage.tile(
-                    [P, TILES * PASSES * P], U8, align_bytes=64, name="x_scales%d" % part, tag="x_scales%d" % part
-                )
-                nc.vector.quantize_mx(
-                    out=x_codes[:].bitcast(FP8X4),
-                    scales=x_scales[:],
-                    in_=x_words[(b, part)][:].rearrange("p t g k j -> p (t g k j)"),
-                )
-                x_mx[(b, part)] = (x_codes, x_scales)
 
             def exponentials(b):
-                e_sb = stage.tile([P, TILES, S], BF16)
+                e_sb = e_pool.tile([P, TILES, S], BF16)
                 for j in range(TILES):
                     col = b * TILES + j
                     nc.scalar.activation(
@@ -259,47 +323,8 @@ def tile_covenantattention_pa_t_kernel(
                 )
                 e_mx[b] = (e_codes, e_scales)
 
-            def values(b):
-                v_ps = [psum.tile([P, TILES, HD], F32, name="bank", tag="bank") for part in (REAL, IMAG)]
-                steps = [(part, g) for part in (REAL, IMAG) for g in range(PASSES)]
-                for t in range(TILES):
-                    for n, (x_part, g) in enumerate(steps):
-                        x_codes, x_scales = x_mx[(b, x_part)]
-                        cols = slice((t * PASSES + g) * P, (t * PASSES + g + 1) * P)
-                        for v_part in (REAL, IMAG):
-                            w = WEIGHT_OF[x_part][v_part]
-                            nc.tensor.matmul_mx(
-                                out=v_ps[v_part][:, t, :],
-                                lhsT=x_codes[:, cols].bitcast(FP8X4),
-                                lhsT_scale=x_scales[:, cols],
-                                rhs=w_codes[:, w, g, :].bitcast(FP8X4),
-                                rhs_scale=w_scales[:, w, g, :],
-                                start=(n == 0),
-                                stop=(n == len(steps) - 1),
-                            )
-                v_grouped = stage.tile([P, 2, HD, PACK], BF16, align_bytes=64)
-                for v_part in (REAL, IMAG):
-                    nc.vector.tensor_tensor(
-                        out=v_grouped[:, v_part],
-                        in0=v_ps[v_part][:].rearrange("p t d -> p d t"),
-                        in1=bias[:, v_part, :].unsqueeze(2).to_broadcast([P, HD, PACK]),
-                        op=ALU.add,
-                    )
-                v_words[b] = v_grouped
-
-            def quantise_v(b):
-                v_codes = stage.tile([P, 2 * HD], U32, align_bytes=64)
-                v_scales = stage.tile([P, 2 * HD], U8, align_bytes=64)
-                nc.vector.quantize_mx(
-                    out=v_codes[:].bitcast(FP8X4),
-                    scales=v_scales[:],
-                    in_=v_words[b][:].rearrange("p c d t -> p (c d t)"),
-                )
-                v_mx[b] = (v_codes, v_scales)
-
             def outputs(b):
                 e_codes, e_scales = e_mx[b]
-                v_codes, v_scales = v_mx[b]
                 cols_b = slice(b * TILES, (b + 1) * TILES)
                 nc.vector.reciprocal(out=inv_sum[:, cols_b], in_=row_sum[:, cols_b])
                 o_sb = stage.tile([P, 2, TILES, HD], F32)
@@ -312,8 +337,8 @@ def tile_covenantattention_pa_t_kernel(
                             out=o_ps[:, jj, :],
                             lhsT=e_codes[:, cols].bitcast(FP8X4),
                             lhsT_scale=e_scales[:, cols],
-                            rhs=v_codes[:].bitcast(FP8X4),
-                            rhs_scale=v_scales[:],
+                            rhs=v_codes[:, b, :].bitcast(FP8X4),
+                            rhs_scale=v_scales[:, b, :],
                             start=True,
                             stop=True,
                         )
@@ -330,30 +355,12 @@ def tile_covenantattention_pa_t_kernel(
                         out=outs[part][b].rearrange("(p j) d -> p j d", j=TILES), in_=o_sb[:, part]
                     )
 
-            flip_x(0, REAL)
-            for j in range(TILES):
-                negated_row_max(B - 1, j)
-            quantise_x(0, REAL)
-            flip_x(0, IMAG)
-            quantise_x(0, IMAG)
-            load_x(X_BUFS)
             exponentials(0)
             for b in range(B):
-                ahead = b + 1
-                if ahead < B:
-                    flip_x(ahead, REAL)
+                if b + 1 < B:
+                    exponentials(b + 1)
                 flip_e(b)
-                if ahead < B:
-                    quantise_x(ahead, REAL)
-                quantise_e(b)
-                if ahead < B:
-                    flip_x(ahead, IMAG)
-                    quantise_x(ahead, IMAG)
-                    if ahead + X_BUFS < B:
-                        load_x(ahead + X_BUFS)
-                    exponentials(ahead)
-                values(b)
                 if b >= 1:
                     outputs(b - 1)
-                quantise_v(b)
+                quantise_e(b)
             outputs(B - 1)

@@ -23,6 +23,7 @@ W_R, W_I, W_NEG_I = 0, 1, 2
 WEIGHT_OF = ((W_R, W_I), (W_NEG_I, W_R))
 X_BUFS = 2
 QK_BUFS = 4
+EARLY = 2
 
 FLOPS = 4 * 2 * B * S * DX * HD + 4 * 2 * B * S * S * HD + 2 * 2 * B * S * S * HD
 
@@ -44,6 +45,8 @@ def tile_covenantattention_pa_t_kernel(
         whole.enter_context(tc.manual_schedule())
         const = whole.enter_context(tc.tile_pool(name="const", bufs=1))
         m_pool = whole.enter_context(tc.tile_pool(name="m_pool", bufs=1))
+        x_pool = whole.enter_context(tc.tile_pool(name="x_pool", bufs=X_BUFS))
+        x_keep = whole.enter_context(tc.tile_pool(name="x_keep", bufs=EARLY + 1))
         psum = whole.enter_context(tc.psum_pool(name="psum", bufs=8))
 
         warm = const.tile([P, 1], F32)
@@ -65,8 +68,54 @@ def tile_covenantattention_pa_t_kernel(
         w_grouped = const.tile([P, 3, PASSES, HD, PACK], BF16, align_bytes=64)
         w_codes = const.tile([P, 3, PASSES, HD], U32, align_bytes=64)
         w_scales = const.tile([P, 3, PASSES, HD], U8, align_bytes=64)
-        v_codes = const.tile([P, B, 2 * HD], U32, align_bytes=64)
-        v_scales = const.tile([P, B, 2 * HD], U8, align_bytes=64)
+        x_nat = {}
+        x_words = {}
+        x_mx = {}
+
+        def load_x(b):
+            for part in (REAL, IMAG):
+                x_sb = x_pool.tile([P, TILES, DX], BF16, name="x_sb%d" % part, tag="x_sb%d" % part)
+                nc.sync.dma_start(
+                    out=x_sb[:], in_=x_parts[part][b].rearrange("(p t) f -> p t f", t=TILES)
+                )
+                x_nat[(b, part)] = x_sb
+
+        def flip_x_tile(b, part, t, copy):
+            bank = psum.tile([P, BLOCKS, P], F32, name="bank", tag="bank")
+            transpose_words(nc, bank, x_nat[(b, part)][:, t, :], ident_f32)
+            copy(
+                out=x_words[(b, part)][:, t].bitcast(F32),
+                in_=bank[:].rearrange("p (g u) k -> p g k u", u=2),
+            )
+
+        def quantise_x(b, part):
+            x_codes = x_keep.tile(
+                [P, TILES * PASSES * P], U32, align_bytes=64, name="x_codes%d" % part, tag="x_codes%d" % part
+            )
+            x_scales = x_keep.tile(
+                [P, TILES * PASSES * P], U8, align_bytes=64, name="x_scales%d" % part, tag="x_scales%d" % part
+            )
+            nc.vector.quantize_mx(
+                out=x_codes[:].bitcast(FP8X4),
+                scales=x_scales[:],
+                in_=x_words[(b, part)][:].rearrange("p t g k j -> p (t g k j)"),
+            )
+            x_mx[(b, part)] = (x_codes, x_scales)
+
+        def quantise_weights():
+            for w in range(3):
+                bank = psum.tile([P, BLOCKS, P], F32, name="bank", tag="bank")
+                transpose_words(nc, bank, w_nat[:, w, :], ident_f32)
+                nc.vector.tensor_copy(
+                    out=w_grouped[:, w].bitcast(F32),
+                    in_=bank[:].rearrange("p (g u) d -> p g d u", u=2),
+                )
+            for w in range(3):
+                nc.vector.quantize_mx(
+                    out=w_codes[:, w].rearrange("p g d -> p (g d)").bitcast(FP8X4),
+                    scales=w_scales[:, w].rearrange("p g d -> p (g d)"),
+                    in_=w_grouped[:, w].rearrange("p g d j -> p (g d j)"),
+                )
 
         def magnitudes(b):
             flat = m_tiles[b][:].rearrange("p j s -> p (j s)")
@@ -79,27 +128,13 @@ def tile_covenantattention_pa_t_kernel(
             )
 
         with ExitStack() as phase:
-            x_pool = phase.enter_context(tc.tile_pool(name="x_pool", bufs=X_BUFS))
             nat = phase.enter_context(tc.tile_pool(name="nat", bufs=QK_BUFS))
-            flipped = phase.enter_context(tc.tile_pool(name="flipped", bufs=2))
+            flipped = phase.enter_context(tc.tile_pool(name="flipped", bufs=3))
             squares = phase.enter_context(tc.tile_pool(name="squares", bufs=3))
-            x_stage = phase.enter_context(tc.tile_pool(name="x_stage", bufs=3))
-            x_keep = phase.enter_context(tc.tile_pool(name="x_keep", bufs=2))
+            early = phase.enter_context(tc.tile_pool(name="early", bufs=1))
 
-            x_nat = {}
             qk_nat = {}
             qk_t = {}
-            x_words = {}
-            x_mx = {}
-            v_words = {}
-
-            def load_x(b):
-                for part in (REAL, IMAG):
-                    x_sb = x_pool.tile([P, TILES, DX], BF16, name="x_sb%d" % part, tag="x_sb%d" % part)
-                    nc.sync.dma_start(
-                        out=x_sb[:], in_=x_parts[part][b].rearrange("(p t) f -> p t f", t=TILES)
-                    )
-                    x_nat[(b, part)] = x_sb
 
             def load_qk(b):
                 q_nat = nat.tile([P, 2, TILES, HD], BF16)
@@ -113,22 +148,6 @@ def tile_covenantattention_pa_t_kernel(
                         out=k_nat[:, part], in_=src[b, 0].rearrange("(p t) d -> p t d", t=TILES)
                     )
                 qk_nat[b] = (q_nat, k_nat)
-
-            def quantise_weights():
-                nc.vector.tensor_scalar_mul(out=w_nat[:, W_NEG_I, :], in0=w_nat[:, W_I, :], scalar1=-1.0)
-                for w in range(3):
-                    bank = psum.tile([P, BLOCKS, P], F32, name="bank", tag="bank")
-                    transpose_words(nc, bank, w_nat[:, w, :], ident_f32)
-                    nc.vector.tensor_copy(
-                        out=w_grouped[:, w].bitcast(F32),
-                        in_=bank[:].rearrange("p (g u) d -> p g d u", u=2),
-                    )
-                for w in range(3):
-                    nc.vector.quantize_mx(
-                        out=w_codes[:, w].rearrange("p g d -> p (g d)").bitcast(FP8X4),
-                        scales=w_scales[:, w].rearrange("p g d -> p (g d)"),
-                        in_=w_grouped[:, w].rearrange("p g d j -> p (g d j)"),
-                    )
 
             def flip_qk(b):
                 q_nat, k_nat = qk_nat[b]
@@ -158,137 +177,85 @@ def tile_covenantattention_pa_t_kernel(
                 if b + QK_BUFS < B:
                     load_qk(b + QK_BUFS)
 
-            def scores_and_x(b, j):
+            def squared_magnitudes(b, j):
                 q_t, neg_qi_t, k_t = qk_t[b]
                 cols = slice(j * P, (j + 1) * P)
                 s_r = psum.tile([P, S], F32, name="bank", tag="bank")
-                x_r = psum.tile([P, BLOCKS, P], F32, name="bank", tag="bank")
                 s_i = psum.tile([P, S], F32, name="bank", tag="bank")
-                x_i = psum.tile([P, BLOCKS, P], F32, name="bank", tag="bank")
-                products = (
-                    (s_r, q_t[:, REAL, cols], REAL, x_r),
-                    (s_r, neg_qi_t[:, cols], IMAG, x_r),
-                    (s_i, q_t[:, REAL, cols], IMAG, x_i),
-                    (s_i, q_t[:, IMAG, cols], REAL, x_i),
-                )
-                for n, (acc, q_cols, k_part, x_bank) in enumerate(products):
-                    second = n % 2
-                    nc.tensor.matmul(
-                        acc[:], lhsT=q_cols, rhs=k_t[:, k_part, :], start=(second == 0), stop=(second == 1)
-                    )
-                    words = x_nat[(b, n // 2)][:, j, :].bitcast(F32)
-                    for i in (2 * second, 2 * second + 1):
-                        nc.tensor.transpose(x_bank[:, i, :], words[:, i * P : (i + 1) * P], ident_f32[:])
+                nc.tensor.matmul(s_r[:], lhsT=q_t[:, REAL, cols], rhs=k_t[:, REAL, :], start=True, stop=False)
+                nc.tensor.matmul(s_r[:], lhsT=neg_qi_t[:, cols], rhs=k_t[:, IMAG, :], start=False, stop=True)
+                nc.tensor.matmul(s_i[:], lhsT=q_t[:, REAL, cols], rhs=k_t[:, IMAG, :], start=True, stop=False)
+                nc.tensor.matmul(s_i[:], lhsT=q_t[:, IMAG, cols], rhs=k_t[:, REAL, :], start=False, stop=True)
                 sq_r = squares.tile([P, S], F32)
                 sq_i = squares.tile([P, S], F32)
-                x_grouped = x_stage.tile([P, 2, PASSES, P, PACK], BF16, align_bytes=64)
                 nc.scalar.activation(out=sq_r[:], in_=s_r[:], func=ACT.Square)
-                nc.scalar.copy(
-                    out=x_grouped[:, REAL].bitcast(F32), in_=x_r[:].rearrange("p (g u) k -> p g k u", u=2)
-                )
                 nc.scalar.activation(out=sq_i[:], in_=s_i[:], func=ACT.Square)
-                nc.scalar.copy(
-                    out=x_grouped[:, IMAG].bitcast(F32), in_=x_i[:].rearrange("p (g u) k -> p g k u", u=2)
-                )
-                nc.vector.tensor_tensor(out=m_tiles[b][:, j, :], in0=sq_r[:], in1=sq_i[:], op=ALU.add)
-                x_words[(b, j)] = x_grouped
-
-            def quantise_x(b, j):
-                if j == 0:
-                    x_codes = x_keep.tile([P, TILES, 2, PASSES, P], U32, align_bytes=64)
-                    x_scales = x_keep.tile([P, TILES, 2, PASSES, P], U8, align_bytes=64)
-                    x_mx[b] = (x_codes, x_scales)
-                x_codes, x_scales = x_mx[b]
-                nc.vector.quantize_mx(
-                    out=x_codes[:, j].rearrange("p c g k -> p (c g k)").bitcast(FP8X4),
-                    scales=x_scales[:, j].rearrange("p c g k -> p (c g k)"),
-                    in_=x_words[(b, j)][:].rearrange("p c g k t -> p (c g k t)"),
-                )
-
-            def values(b):
-                x_codes, x_scales = x_mx[b]
-                v_ps = [psum.tile([P, TILES, HD], F32, name="bank", tag="bank") for part in (REAL, IMAG)]
-                steps = [(part, g) for part in (REAL, IMAG) for g in range(PASSES)]
-                for t in range(TILES):
-                    for n, (x_part, g) in enumerate(steps):
-                        for v_part in (REAL, IMAG):
-                            w = WEIGHT_OF[x_part][v_part]
-                            nc.tensor.matmul_mx(
-                                out=v_ps[v_part][:, t, :],
-                                lhsT=x_codes[:, t, x_part, g, :].bitcast(FP8X4),
-                                lhsT_scale=x_scales[:, t, x_part, g, :],
-                                rhs=w_codes[:, w, g, :].bitcast(FP8X4),
-                                rhs_scale=w_scales[:, w, g, :],
-                                start=(n == 0),
-                                stop=(n == len(steps) - 1),
-                            )
-                v_grouped = x_stage.tile([P, 2, HD, PACK], BF16, align_bytes=64)
-                for v_part in (REAL, IMAG):
-                    nc.vector.tensor_tensor(
-                        out=v_grouped[:, v_part],
-                        in0=v_ps[v_part][:].rearrange("p t d -> p d t"),
-                        in1=bias[:, v_part, :].unsqueeze(2).to_broadcast([P, HD, PACK]),
-                        op=ALU.add,
-                    )
-                v_words[b] = v_grouped
-
-            def quantise_v(b):
-                nc.vector.quantize_mx(
-                    out=v_codes[:, b, :].bitcast(FP8X4),
-                    scales=v_scales[:, b, :],
-                    in_=v_words[b][:].rearrange("p c d t -> p (c d t)"),
-                )
+                nc.gpsimd.tensor_tensor(out=m_tiles[b][:, j, :], in0=sq_r[:], in1=sq_i[:], op=ALU.add)
 
             load_qk(0)
-            load_x(0)
             load_qk(1)
-            nc.sync.dma_start(out=w_nat[:, W_R, :], in_=wv_r)
-            nc.sync.dma_start(out=w_nat[:, W_I, :], in_=wv_i)
-            load_x(1)
+            load_x(0)
             for b in range(2, QK_BUFS):
                 load_qk(b)
+            nc.sync.dma_start(out=w_nat[:, W_R, :], in_=wv_r)
+            nc.sync.dma_start(out=w_nat[:, W_I, :], in_=wv_i)
             nc.sync.dma_start(out=bias[:, REAL, :], in_=bv_r.partition_broadcast(P))
             nc.sync.dma_start(out=bias[:, IMAG, :], in_=bv_i.partition_broadcast(P))
+            load_x(1)
+            for b in range(EARLY):
+                for part in (REAL, IMAG):
+                    x_words[(b, part)] = early.tile(
+                        [P, TILES, PASSES, P, PACK], BF16, align_bytes=64, name="x_early%d%d" % (b, part)
+                    )
 
             flip_qk(0)
+            flip_qk(1)
             for b in range(B):
                 for j in range(TILES):
-                    scores_and_x(b, j)
+                    squared_magnitudes(b, j)
                     if b >= 2:
                         negated_row_max(b - 2, j)
-                    if j >= 1:
-                        quantise_x(b, j - 1)
-                    if b >= 1 and j == 1:
-                        values(b - 1)
-                    if b + 1 < B and j == 2:
-                        flip_qk(b + 1)
-                    if b >= 1 and j == 3:
-                        quantise_v(b - 1)
-                quantise_x(b, TILES - 1)
-                if b + X_BUFS < B:
-                    load_x(b + X_BUFS)
+                    step = b * TILES + j
+                    if step % 2 == 1:
+                        x_tile = step // 2
+                        x_b, x_part, x_t = x_tile // (2 * TILES), (x_tile // TILES) % 2, x_tile % TILES
+                        flip_x_tile(x_b, x_part, x_t, nc.vector.tensor_copy)
+                        if x_part == IMAG and x_t == TILES - 1:
+                            load_x(x_b + X_BUFS)
                 if b == 0:
+                    nc.vector.tensor_scalar_mul(out=w_nat[:, W_NEG_I, :], in0=w_nat[:, W_I, :], scalar1=-1.0)
+                if b + 2 < B:
+                    flip_qk(b + 2)
+                if b + 2 == B:
                     quantise_weights()
                 if b >= 1:
                     magnitudes(b - 1)
             magnitudes(B - 1)
-            values(B - 1)
-            for j in range(TILES):
-                negated_row_max(B - 2, j)
-            quantise_v(B - 1)
-            for j in range(TILES):
-                negated_row_max(B - 1, j)
+            for b in range(EARLY):
+                for part in (REAL, IMAG):
+                    quantise_x(b, part)
+            for b in (B - 2, B - 1):
+                for j in range(TILES):
+                    negated_row_max(b, j)
 
-        with ExitStack() as phase:
-            stage = phase.enter_context(tc.tile_pool(name="stage", bufs=2, reuse_waits="tile"))
-            e_pool = phase.enter_context(tc.tile_pool(name="e_pool", bufs=3, reuse_waits="tile"))
+        with ExitStack() as era:
+            stage = era.enter_context(tc.tile_pool(name="stage", bufs=2, reuse_waits="tile"))
 
             e_rows = {}
             e_words = {}
             e_mx = {}
+            v_words = {}
+            v_mx = {}
+
+            def flip_x(b, part):
+                x_words[(b, part)] = stage.tile(
+                    [P, TILES, PASSES, P, PACK], BF16, align_bytes=64, name="x_grouped", tag="x_grouped"
+                )
+                for t in range(TILES):
+                    flip_x_tile(b, part, t, nc.scalar.copy)
 
             def exponentials(b):
-                e_sb = e_pool.tile([P, TILES, S], BF16)
+                e_sb = stage.tile([P, TILES, S], BF16)
                 for j in range(TILES):
                     col = b * TILES + j
                     nc.scalar.activation(
@@ -307,7 +274,7 @@ def tile_covenantattention_pa_t_kernel(
                     bank = psum.tile([P, 2, 2, P], F32, name="bank", tag="bank")
                     for jj in range(2):
                         transpose_words(nc, bank[:, jj], e_sb[:, 2 * half + jj, :], ident_f32)
-                    nc.vector.tensor_copy(
+                    nc.scalar.copy(
                         out=e_grouped[:, 2 * half : 2 * half + 2].bitcast(F32),
                         in_=bank[:].rearrange("p j u q -> p j q u"),
                     )
@@ -323,8 +290,47 @@ def tile_covenantattention_pa_t_kernel(
                 )
                 e_mx[b] = (e_codes, e_scales)
 
+            def values(b):
+                v_ps = [psum.tile([P, TILES, HD], F32, name="bank", tag="bank") for part in (REAL, IMAG)]
+                steps = [(part, g) for part in (REAL, IMAG) for g in range(PASSES)]
+                for t in range(TILES):
+                    for n, (x_part, g) in enumerate(steps):
+                        x_codes, x_scales = x_mx[(b, x_part)]
+                        cols = slice((t * PASSES + g) * P, (t * PASSES + g + 1) * P)
+                        for v_part in (REAL, IMAG):
+                            w = WEIGHT_OF[x_part][v_part]
+                            nc.tensor.matmul_mx(
+                                out=v_ps[v_part][:, t, :],
+                                lhsT=x_codes[:, cols].bitcast(FP8X4),
+                                lhsT_scale=x_scales[:, cols],
+                                rhs=w_codes[:, w, g, :].bitcast(FP8X4),
+                                rhs_scale=w_scales[:, w, g, :],
+                                start=(n == 0),
+                                stop=(n == len(steps) - 1),
+                            )
+                v_grouped = stage.tile([P, 2, HD, PACK], BF16, align_bytes=64)
+                for v_part in (REAL, IMAG):
+                    nc.vector.tensor_tensor(
+                        out=v_grouped[:, v_part],
+                        in0=v_ps[v_part][:].rearrange("p t d -> p d t"),
+                        in1=bias[:, v_part, :].unsqueeze(2).to_broadcast([P, HD, PACK]),
+                        op=ALU.add,
+                    )
+                v_words[b] = v_grouped
+
+            def quantise_v(b):
+                v_codes = stage.tile([P, 2 * HD], U32, align_bytes=64)
+                v_scales = stage.tile([P, 2 * HD], U8, align_bytes=64)
+                nc.vector.quantize_mx(
+                    out=v_codes[:].bitcast(FP8X4),
+                    scales=v_scales[:],
+                    in_=v_words[b][:].rearrange("p c d t -> p (c d t)"),
+                )
+                v_mx[b] = (v_codes, v_scales)
+
             def outputs(b):
                 e_codes, e_scales = e_mx[b]
+                v_codes, v_scales = v_mx[b]
                 cols_b = slice(b * TILES, (b + 1) * TILES)
                 nc.vector.reciprocal(out=inv_sum[:, cols_b], in_=row_sum[:, cols_b])
                 o_sb = stage.tile([P, 2, TILES, HD], F32)
@@ -337,8 +343,8 @@ def tile_covenantattention_pa_t_kernel(
                             out=o_ps[:, jj, :],
                             lhsT=e_codes[:, cols].bitcast(FP8X4),
                             lhsT_scale=e_scales[:, cols],
-                            rhs=v_codes[:, b, :].bitcast(FP8X4),
-                            rhs_scale=v_scales[:, b, :],
+                            rhs=v_codes[:].bitcast(FP8X4),
+                            rhs_scale=v_scales[:],
                             start=True,
                             stop=True,
                         )
@@ -356,11 +362,24 @@ def tile_covenantattention_pa_t_kernel(
                     )
 
             exponentials(0)
+            values(0)
+            quantise_v(0)
             for b in range(B):
+                ahead = b + EARLY
+                if ahead < B:
+                    flip_x(ahead, REAL)
+                flip_e(b)
+                if ahead < B:
+                    quantise_x(ahead, REAL)
+                quantise_e(b)
+                if ahead < B:
+                    flip_x(ahead, IMAG)
+                    quantise_x(ahead, IMAG)
+                    if ahead + X_BUFS < B:
+                        load_x(ahead + X_BUFS)
                 if b + 1 < B:
                     exponentials(b + 1)
-                flip_e(b)
-                if b >= 1:
-                    outputs(b - 1)
-                quantise_e(b)
-            outputs(B - 1)
+                    values(b + 1)
+                outputs(b)
+                if b + 1 < B:
+                    quantise_v(b + 1)

@@ -23,7 +23,10 @@ W_R, W_I, W_NEG_I = 0, 1, 2
 WEIGHT_OF = ((W_R, W_I), (W_NEG_I, W_R))
 X_BUFS = 2
 QK_BUFS = 4
-EARLY = 2
+X_TILES = B * 2 * TILES
+X_START = 4
+X_ROUND = 6
+X_VECTOR = 3
 
 FLOPS = 4 * 2 * B * S * DX * HD + 4 * 2 * B * S * S * HD + 2 * 2 * B * S * S * HD
 
@@ -46,7 +49,8 @@ def tile_covenantattention_pa_t_kernel(
         const = whole.enter_context(tc.tile_pool(name="const", bufs=1))
         m_pool = whole.enter_context(tc.tile_pool(name="m_pool", bufs=1))
         x_pool = whole.enter_context(tc.tile_pool(name="x_pool", bufs=X_BUFS))
-        x_keep = whole.enter_context(tc.tile_pool(name="x_keep", bufs=EARLY + 1))
+        x_keep = whole.enter_context(tc.tile_pool(name="x_keep", bufs=5))
+        x_stage = whole.enter_context(tc.tile_pool(name="x_stage", bufs=3))
         psum = whole.enter_context(tc.psum_pool(name="psum", bufs=8))
 
         warm = const.tile([P, 1], F32)
@@ -72,21 +76,25 @@ def tile_covenantattention_pa_t_kernel(
         x_words = {}
         x_mx = {}
 
-        def load_x(b):
-            for part in (REAL, IMAG):
-                x_sb = x_pool.tile([P, TILES, DX], BF16, name="x_sb%d" % part, tag="x_sb%d" % part)
-                nc.sync.dma_start(
-                    out=x_sb[:], in_=x_parts[part][b].rearrange("(p t) f -> p t f", t=TILES)
-                )
-                x_nat[(b, part)] = x_sb
+        def load_x(b, part):
+            x_sb = x_pool.tile([P, TILES, DX], BF16, name="x_sb%d" % part, tag="x_sb%d" % part)
+            nc.sync.dma_start(out=x_sb[:], in_=x_parts[part][b].rearrange("(p t) f -> p t f", t=TILES))
+            x_nat[(b, part)] = x_sb
 
-        def flip_x_tile(b, part, t, copy):
+        def flip_x_tile(i, copy):
+            b, part, t = i // (2 * TILES), (i // TILES) % 2, i % TILES
+            if t == 0:
+                x_words[(b, part)] = x_stage.tile(
+                    [P, TILES, PASSES, P, PACK], BF16, align_bytes=64, name="x_grouped", tag="x_grouped"
+                )
             bank = psum.tile([P, BLOCKS, P], F32, name="bank", tag="bank")
             transpose_words(nc, bank, x_nat[(b, part)][:, t, :], ident_f32)
             copy(
                 out=x_words[(b, part)][:, t].bitcast(F32),
                 in_=bank[:].rearrange("p (g u) k -> p g k u", u=2),
             )
+            if t == TILES - 1 and b + X_BUFS < B:
+                load_x(b + X_BUFS, part)
 
         def quantise_x(b, part):
             x_codes = x_keep.tile(
@@ -131,7 +139,6 @@ def tile_covenantattention_pa_t_kernel(
             nat = phase.enter_context(tc.tile_pool(name="nat", bufs=QK_BUFS))
             flipped = phase.enter_context(tc.tile_pool(name="flipped", bufs=3))
             squares = phase.enter_context(tc.tile_pool(name="squares", bufs=3))
-            early = phase.enter_context(tc.tile_pool(name="early", bufs=1))
 
             qk_nat = {}
             qk_t = {}
@@ -186,27 +193,24 @@ def tile_covenantattention_pa_t_kernel(
                 nc.tensor.matmul(s_r[:], lhsT=neg_qi_t[:, cols], rhs=k_t[:, IMAG, :], start=False, stop=True)
                 nc.tensor.matmul(s_i[:], lhsT=q_t[:, REAL, cols], rhs=k_t[:, IMAG, :], start=True, stop=False)
                 nc.tensor.matmul(s_i[:], lhsT=q_t[:, IMAG, cols], rhs=k_t[:, REAL, :], start=False, stop=True)
-                sq_r = squares.tile([P, S], F32)
                 sq_i = squares.tile([P, S], F32)
-                nc.scalar.activation(out=sq_r[:], in_=s_r[:], func=ACT.Square)
+                m_row = m_tiles[b][:, j, :]
+                nc.scalar.activation(out=m_row, in_=s_r[:], func=ACT.Square)
                 nc.scalar.activation(out=sq_i[:], in_=s_i[:], func=ACT.Square)
-                nc.gpsimd.tensor_tensor(out=m_tiles[b][:, j, :], in0=sq_r[:], in1=sq_i[:], op=ALU.add)
+                nc.gpsimd.tensor_tensor(out=m_row, in0=m_row, in1=sq_i[:], op=ALU.add)
 
             load_qk(0)
             load_qk(1)
-            load_x(0)
+            for part in (REAL, IMAG):
+                load_x(0, part)
             for b in range(2, QK_BUFS):
                 load_qk(b)
             nc.sync.dma_start(out=w_nat[:, W_R, :], in_=wv_r)
             nc.sync.dma_start(out=w_nat[:, W_I, :], in_=wv_i)
             nc.sync.dma_start(out=bias[:, REAL, :], in_=bv_r.partition_broadcast(P))
             nc.sync.dma_start(out=bias[:, IMAG, :], in_=bv_i.partition_broadcast(P))
-            load_x(1)
-            for b in range(EARLY):
-                for part in (REAL, IMAG):
-                    x_words[(b, part)] = early.tile(
-                        [P, TILES, PASSES, P, PACK], BF16, align_bytes=64, name="x_early%d%d" % (b, part)
-                    )
+            for part in (REAL, IMAG):
+                load_x(1, part)
 
             flip_qk(0)
             flip_qk(1)
@@ -216,12 +220,12 @@ def tile_covenantattention_pa_t_kernel(
                     if b >= 2:
                         negated_row_max(b - 2, j)
                     step = b * TILES + j
-                    if step % 2 == 1:
-                        x_tile = step // 2
-                        x_b, x_part, x_t = x_tile // (2 * TILES), (x_tile // TILES) % 2, x_tile % TILES
-                        flip_x_tile(x_b, x_part, x_t, nc.vector.tensor_copy)
-                        if x_part == IMAG and x_t == TILES - 1:
-                            load_x(x_b + X_BUFS)
+                    x_tile = step - X_START
+                    if x_tile >= 0:
+                        flip_x_tile(x_tile, nc.vector.tensor_copy)
+                    if x_tile >= TILES and x_tile % TILES == 1:
+                        group = x_tile // TILES - 1
+                        quantise_x(group // 2, group % 2)
                 if b == 0:
                     nc.vector.tensor_scalar_mul(out=w_nat[:, W_NEG_I, :], in0=w_nat[:, W_I, :], scalar1=-1.0)
                 if b + 2 < B:
@@ -231,9 +235,8 @@ def tile_covenantattention_pa_t_kernel(
                 if b >= 1:
                     magnitudes(b - 1)
             magnitudes(B - 1)
-            for b in range(EARLY):
-                for part in (REAL, IMAG):
-                    quantise_x(b, part)
+            x_done = B * TILES - X_START
+            groups_done = x_done // TILES - 1
             for b in (B - 2, B - 1):
                 for j in range(TILES):
                     negated_row_max(b, j)
@@ -246,13 +249,6 @@ def tile_covenantattention_pa_t_kernel(
             e_mx = {}
             v_words = {}
             v_mx = {}
-
-            def flip_x(b, part):
-                x_words[(b, part)] = stage.tile(
-                    [P, TILES, PASSES, P, PACK], BF16, align_bytes=64, name="x_grouped", tag="x_grouped"
-                )
-                for t in range(TILES):
-                    flip_x_tile(b, part, t, nc.scalar.copy)
 
             def exponentials(b):
                 e_sb = stage.tile([P, TILES, S], BF16)
@@ -365,18 +361,14 @@ def tile_covenantattention_pa_t_kernel(
             values(0)
             quantise_v(0)
             for b in range(B):
-                ahead = b + EARLY
-                if ahead < B:
-                    flip_x(ahead, REAL)
+                while groups_done < x_done // TILES:
+                    quantise_x(groups_done // 2, groups_done % 2)
+                    groups_done += 1
+                for i in range(x_done, min(x_done + X_ROUND, X_TILES)):
+                    flip_x_tile(i, nc.vector.tensor_copy if i % X_VECTOR == X_VECTOR - 1 else nc.scalar.copy)
+                x_done = min(x_done + X_ROUND, X_TILES)
                 flip_e(b)
-                if ahead < B:
-                    quantise_x(ahead, REAL)
                 quantise_e(b)
-                if ahead < B:
-                    flip_x(ahead, IMAG)
-                    quantise_x(ahead, IMAG)
-                    if ahead + X_BUFS < B:
-                        load_x(ahead + X_BUFS)
                 if b + 1 < B:
                     exponentials(b + 1)
                     values(b + 1)

@@ -24,9 +24,16 @@ WEIGHT_OF = ((W_R, W_I), (W_NEG_I, W_R))
 X_BUFS = 2
 QK_BUFS = 4
 X_TILES = B * 2 * TILES
+X_EARLY = 28
 X_START = 4
-X_ROUND = 6
+X_HALF = (3, 3)
+V_LEAD = 2
+ROOT_ROWS = 2
+FLIP_AT = 1
+W_AT = 8
+MAX_LAG = 12
 X_VECTOR = 3
+HALVES = ((0, 1), (2, 3))
 
 FLOPS = 4 * 2 * B * S * DX * HD + 4 * 2 * B * S * S * HD + 2 * 2 * B * S * S * HD
 
@@ -51,7 +58,8 @@ def tile_covenantattention_pa_t_kernel(
         x_pool = whole.enter_context(tc.tile_pool(name="x_pool", bufs=X_BUFS))
         x_keep = whole.enter_context(tc.tile_pool(name="x_keep", bufs=5))
         x_stage = whole.enter_context(tc.tile_pool(name="x_stage", bufs=3))
-        psum = whole.enter_context(tc.psum_pool(name="psum", bufs=8))
+        mm_psum = whole.enter_context(tc.psum_pool(name="mm_psum", bufs=4))
+        tr_psum = whole.enter_context(tc.psum_pool(name="tr_psum", bufs=4))
 
         warm = const.tile([P, 1], F32)
         nc.vector.memset(warm[:], 1.0)
@@ -87,7 +95,7 @@ def tile_covenantattention_pa_t_kernel(
                 x_words[(b, part)] = x_stage.tile(
                     [P, TILES, PASSES, P, PACK], BF16, align_bytes=64, name="x_grouped", tag="x_grouped"
                 )
-            bank = psum.tile([P, BLOCKS, P], F32, name="bank", tag="bank")
+            bank = tr_psum.tile([P, BLOCKS, P], F32, name="bank", tag="bank")
             transpose_words(nc, bank, x_nat[(b, part)][:, t, :], ident_f32)
             copy(
                 out=x_words[(b, part)][:, t].bitcast(F32),
@@ -111,8 +119,9 @@ def tile_covenantattention_pa_t_kernel(
             x_mx[(b, part)] = (x_codes, x_scales)
 
         def quantise_weights():
+            nc.vector.tensor_scalar_mul(out=w_nat[:, W_NEG_I, :], in0=w_nat[:, W_I, :], scalar1=-1.0)
             for w in range(3):
-                bank = psum.tile([P, BLOCKS, P], F32, name="bank", tag="bank")
+                bank = tr_psum.tile([P, BLOCKS, P], F32, name="bank", tag="bank")
                 transpose_words(nc, bank, w_nat[:, w, :], ident_f32)
                 nc.vector.tensor_copy(
                     out=w_grouped[:, w].bitcast(F32),
@@ -125,14 +134,18 @@ def tile_covenantattention_pa_t_kernel(
                     in_=w_grouped[:, w].rearrange("p g d j -> p (g d j)"),
                 )
 
-        def magnitudes(b):
-            flat = m_tiles[b][:].rearrange("p j s -> p (j s)")
+        def magnitudes(row):
+            b, j = row // TILES, row % TILES
+            flat = m_tiles[b][:, j : j + ROOT_ROWS].rearrange("p j s -> p (j s)")
             nc.scalar.activation(out=flat, in_=flat, func=ACT.Sqrt, scale=1.0 / HD)
 
-        def negated_row_max(b, j):
-            col = b * TILES + j
+        def negated_row_max(row):
             nc.vector.tensor_reduce(
-                out=neg_max[:, col : col + 1], in_=m_tiles[b][:, j, :], axis=AXIS.X, op=ALU.max, negate=True
+                out=neg_max[:, row : row + 1],
+                in_=m_tiles[row // TILES][:, row % TILES, :],
+                axis=AXIS.X,
+                op=ALU.max,
+                negate=True,
             )
 
         with ExitStack() as phase:
@@ -158,8 +171,8 @@ def tile_covenantattention_pa_t_kernel(
 
             def flip_qk(b):
                 q_nat, k_nat = qk_nat[b]
-                q_ps = psum.tile([P, 2, TILES, P], BF16, name="bank", tag="bank")
-                k_ps = psum.tile([P, 2, TILES, P], BF16, name="bank", tag="bank")
+                q_ps = tr_psum.tile([P, 2, TILES, P], BF16, name="bank", tag="bank")
+                k_ps = tr_psum.tile([P, 2, TILES, P], BF16, name="bank", tag="bank")
                 for part in (REAL, IMAG):
                     for j in range(TILES):
                         nc.tensor.transpose(q_ps[:, part, j, :], q_nat[:, part, j, :], ident_bf[:])
@@ -173,8 +186,8 @@ def tile_covenantattention_pa_t_kernel(
                     out=q_t[:].rearrange("d c s -> d (c s)"),
                     in_=q_ps[:].rearrange("d c j p -> d (c j p)"),
                 )
-                nc.vector.tensor_scalar_mul(
-                    out=neg_qi_t[:], in0=q_ps[:, IMAG].rearrange("d j p -> d (j p)"), scalar1=-1.0
+                nc.gpsimd.tensor_scalar(
+                    out=neg_qi_t[:], in0=q_t[:, IMAG, :], scalar1=-1.0, scalar2=0.0, op0=ALU.mult, op1=ALU.add
                 )
                 nc.vector.tensor_copy(
                     out=k_t[:].rearrange("d c (u p e) -> d (c u) p e", u=2, e=2),
@@ -187,8 +200,8 @@ def tile_covenantattention_pa_t_kernel(
             def squared_magnitudes(b, j):
                 q_t, neg_qi_t, k_t = qk_t[b]
                 cols = slice(j * P, (j + 1) * P)
-                s_r = psum.tile([P, S], F32, name="bank", tag="bank")
-                s_i = psum.tile([P, S], F32, name="bank", tag="bank")
+                s_r = mm_psum.tile([P, S], F32, name="bank", tag="bank")
+                s_i = mm_psum.tile([P, S], F32, name="bank", tag="bank")
                 nc.tensor.matmul(s_r[:], lhsT=q_t[:, REAL, cols], rhs=k_t[:, REAL, :], start=True, stop=False)
                 nc.tensor.matmul(s_r[:], lhsT=neg_qi_t[:, cols], rhs=k_t[:, IMAG, :], start=False, stop=True)
                 nc.tensor.matmul(s_i[:], lhsT=q_t[:, REAL, cols], rhs=k_t[:, IMAG, :], start=True, stop=False)
@@ -213,68 +226,68 @@ def tile_covenantattention_pa_t_kernel(
                 load_x(1, part)
 
             flip_qk(0)
-            flip_qk(1)
             for b in range(B):
                 for j in range(TILES):
                     squared_magnitudes(b, j)
-                    if b >= 2:
-                        negated_row_max(b - 2, j)
                     step = b * TILES + j
+                    if step >= MAX_LAG:
+                        negated_row_max(step - MAX_LAG)
+                    if step > ROOT_ROWS and step % ROOT_ROWS == ROOT_ROWS - 1:
+                        magnitudes(step - 2 * ROOT_ROWS + 1)
+                    if step % TILES == FLIP_AT and b + 1 < B:
+                        flip_qk(b + 1)
+                    if step == W_AT:
+                        quantise_weights()
                     x_tile = step - X_START
-                    if x_tile >= 0:
+                    if 0 <= x_tile < X_EARLY:
                         flip_x_tile(x_tile, nc.vector.tensor_copy)
-                    if x_tile >= TILES and x_tile % TILES == 1:
+                    if TILES <= x_tile < X_EARLY and x_tile % TILES == 1:
                         group = x_tile // TILES - 1
                         quantise_x(group // 2, group % 2)
-                if b == 0:
-                    nc.vector.tensor_scalar_mul(out=w_nat[:, W_NEG_I, :], in0=w_nat[:, W_I, :], scalar1=-1.0)
-                if b + 2 < B:
-                    flip_qk(b + 2)
-                if b + 2 == B:
-                    quantise_weights()
-                if b >= 1:
-                    magnitudes(b - 1)
-            magnitudes(B - 1)
-            x_done = B * TILES - X_START
+            x_done = X_EARLY
             groups_done = x_done // TILES - 1
-            for b in (B - 2, B - 1):
-                for j in range(TILES):
-                    negated_row_max(b, j)
+            magnitudes(B * TILES - ROOT_ROWS)
 
         with ExitStack() as era:
             stage = era.enter_context(tc.tile_pool(name="stage", bufs=2, reuse_waits="tile"))
 
+            e_pool = era.enter_context(tc.tile_pool(name="e_pool", bufs=3, reuse_waits="tile"))
+
             e_rows = {}
             e_words = {}
             e_mx = {}
+            v_banks = {}
             v_words = {}
             v_mx = {}
 
-            def exponentials(b):
-                e_sb = stage.tile([P, TILES, S], BF16)
-                for j in range(TILES):
+            o_tiles = {}
+            o_banks = {}
+
+            def exponentials(b, half):
+                if half == 0:
+                    e_rows[b] = e_pool.tile([P, TILES, S], BF16, name="e_sb", tag="e_sb")
+                for j in HALVES[half]:
                     col = b * TILES + j
                     nc.scalar.activation(
-                        out=e_sb[:, j, :],
+                        out=e_rows[b][:, j, :],
                         in_=m_tiles[b][:, j, :],
                         func=ACT.Exp,
                         bias=neg_max[:, col : col + 1],
                         accum_out=row_sum[:, col : col + 1],
                     )
-                e_rows[b] = e_sb
 
-            def flip_e(b):
-                e_sb = e_rows[b]
-                e_grouped = stage.tile([P, TILES, P, PACK], BF16, align_bytes=64)
-                for half in range(TILES // 2):
-                    bank = psum.tile([P, 2, 2, P], F32, name="bank", tag="bank")
-                    for jj in range(2):
-                        transpose_words(nc, bank[:, jj], e_sb[:, 2 * half + jj, :], ident_f32)
-                    nc.scalar.copy(
-                        out=e_grouped[:, 2 * half : 2 * half + 2].bitcast(F32),
-                        in_=bank[:].rearrange("p j u q -> p j q u"),
+            def flip_e(b, half):
+                if half == 0:
+                    e_words[b] = stage.tile(
+                        [P, TILES, P, PACK], BF16, align_bytes=64, name="e_grouped", tag="e_grouped"
                     )
-                e_words[b] = e_grouped
+                bank = tr_psum.tile([P, 2, 2, P], F32, name="bank", tag="bank")
+                for jj in range(2):
+                    transpose_words(nc, bank[:, jj], e_rows[b][:, 2 * half + jj, :], ident_f32)
+                nc.scalar.copy(
+                    out=e_words[b][:, 2 * half : 2 * half + 2].bitcast(F32),
+                    in_=bank[:].rearrange("p j u q -> p j q u"),
+                )
 
             def quantise_e(b):
                 e_codes = stage.tile([P, S], U32, align_bytes=64)
@@ -286,17 +299,20 @@ def tile_covenantattention_pa_t_kernel(
                 )
                 e_mx[b] = (e_codes, e_scales)
 
-            def values(b):
-                v_ps = [psum.tile([P, TILES, HD], F32, name="bank", tag="bank") for part in (REAL, IMAG)]
+            def values(b, half):
+                if half == 0:
+                    v_banks[b] = [
+                        mm_psum.tile([P, TILES, HD], F32, name="bank", tag="bank") for part in (REAL, IMAG)
+                    ]
                 steps = [(part, g) for part in (REAL, IMAG) for g in range(PASSES)]
-                for t in range(TILES):
+                for t in HALVES[half]:
                     for n, (x_part, g) in enumerate(steps):
                         x_codes, x_scales = x_mx[(b, x_part)]
                         cols = slice((t * PASSES + g) * P, (t * PASSES + g + 1) * P)
                         for v_part in (REAL, IMAG):
                             w = WEIGHT_OF[x_part][v_part]
                             nc.tensor.matmul_mx(
-                                out=v_ps[v_part][:, t, :],
+                                out=v_banks[b][v_part][:, t, :],
                                 lhsT=x_codes[:, cols].bitcast(FP8X4),
                                 lhsT_scale=x_scales[:, cols],
                                 rhs=w_codes[:, w, g, :].bitcast(FP8X4),
@@ -304,19 +320,21 @@ def tile_covenantattention_pa_t_kernel(
                                 start=(n == 0),
                                 stop=(n == len(steps) - 1),
                             )
+
+            def biased_values(b):
                 v_grouped = stage.tile([P, 2, HD, PACK], BF16, align_bytes=64)
                 for v_part in (REAL, IMAG):
                     nc.vector.tensor_tensor(
                         out=v_grouped[:, v_part],
-                        in0=v_ps[v_part][:].rearrange("p t d -> p d t"),
+                        in0=v_banks[b][v_part][:].rearrange("p t d -> p d t"),
                         in1=bias[:, v_part, :].unsqueeze(2).to_broadcast([P, HD, PACK]),
                         op=ALU.add,
                     )
                 v_words[b] = v_grouped
 
             def quantise_v(b):
-                v_codes = stage.tile([P, 2 * HD], U32, align_bytes=64)
-                v_scales = stage.tile([P, 2 * HD], U8, align_bytes=64)
+                v_codes = e_pool.tile([P, 2 * HD], U32, align_bytes=64)
+                v_scales = e_pool.tile([P, 2 * HD], U8, align_bytes=64)
                 nc.vector.quantize_mx(
                     out=v_codes[:].bitcast(FP8X4),
                     scales=v_scales[:],
@@ -324,54 +342,72 @@ def tile_covenantattention_pa_t_kernel(
                 )
                 v_mx[b] = (v_codes, v_scales)
 
-            def outputs(b):
+            def outputs(b, half):
                 e_codes, e_scales = e_mx[b]
                 v_codes, v_scales = v_mx[b]
-                cols_b = slice(b * TILES, (b + 1) * TILES)
-                nc.vector.reciprocal(out=inv_sum[:, cols_b], in_=row_sum[:, cols_b])
-                o_sb = stage.tile([P, 2, TILES, HD], F32)
-                for half in range(TILES // 2):
-                    o_ps = psum.tile([P, 2, 2 * HD], F32, name="bank", tag="bank")
-                    for jj in range(2):
-                        j = 2 * half + jj
-                        cols = slice(j * P, (j + 1) * P)
-                        nc.tensor.matmul_mx(
-                            out=o_ps[:, jj, :],
-                            lhsT=e_codes[:, cols].bitcast(FP8X4),
-                            lhsT_scale=e_scales[:, cols],
-                            rhs=v_codes[:].bitcast(FP8X4),
-                            rhs_scale=v_scales[:],
-                            start=True,
-                            stop=True,
-                        )
-                    for jj in range(2):
-                        j = 2 * half + jj
-                        col = b * TILES + j
-                        nc.vector.tensor_scalar_mul(
-                            out=o_sb[:, :, j, :],
-                            in0=o_ps[:, jj, :].rearrange("p (c d) -> p c d", c=2),
-                            scalar1=inv_sum[:, col : col + 1],
-                        )
-                for part in (REAL, IMAG):
-                    nc.sync.dma_start(
-                        out=outs[part][b].rearrange("(p j) d -> p j d", j=TILES), in_=o_sb[:, part]
+                if half == 0:
+                    cols_b = slice(b * TILES, (b + 1) * TILES)
+                    nc.vector.reciprocal(out=inv_sum[:, cols_b], in_=row_sum[:, cols_b])
+                    o_tiles[b] = stage.tile([P, 2, TILES, HD], F32, name="o_sb", tag="o_sb")
+                o_ps = mm_psum.tile([P, 2, 2 * HD], F32, name="bank", tag="bank")
+                o_banks[b, half] = o_ps
+                for jj, j in enumerate(HALVES[half]):
+                    cols = slice(j * P, (j + 1) * P)
+                    nc.tensor.matmul_mx(
+                        out=o_ps[:, jj, :],
+                        lhsT=e_codes[:, cols].bitcast(FP8X4),
+                        lhsT_scale=e_scales[:, cols],
+                        rhs=v_codes[:].bitcast(FP8X4),
+                        rhs_scale=v_scales[:],
+                        start=True,
+                        stop=True,
                     )
 
-            exponentials(0)
-            values(0)
-            quantise_v(0)
-            for b in range(B):
+            def normalise(b, half):
+                o_sb = o_tiles[b]
+                o_ps = o_banks[b, half]
+                for jj, j in enumerate(HALVES[half]):
+                    col = b * TILES + j
+                    nc.vector.tensor_scalar_mul(
+                        out=o_sb[:, :, j, :],
+                        in0=o_ps[:, jj, :].rearrange("p (c d) -> p c d", c=2),
+                        scalar1=inv_sum[:, col : col + 1],
+                    )
+                if half == 1:
+                    for part in (REAL, IMAG):
+                        nc.sync.dma_start(
+                            out=outs[part][b].rearrange("(p j) d -> p j d", j=TILES), in_=o_sb[:, part]
+                        )
+
+            pending = []
+            for step in range(-4, 2 * B + 2):
+                b, half = step // 2, step % 2
+                for done in pending:
+                    normalise(*done)
+                pending = []
+                for row in range(B * TILES - MAX_LAG + 2 * (step + 4), B * TILES - MAX_LAG + 2 * (step + 5)):
+                    if row < B * TILES:
+                        negated_row_max(row)
+                if half == 0:
+                    if 0 <= b - 1 + V_LEAD < B:
+                        biased_values(b - 1 + V_LEAD)
+                    if 0 <= b < B:
+                        quantise_e(b)
+                elif 0 <= b - 1 + V_LEAD < B:
+                    quantise_v(b - 1 + V_LEAD)
                 while groups_done < x_done // TILES:
                     quantise_x(groups_done // 2, groups_done % 2)
                     groups_done += 1
-                for i in range(x_done, min(x_done + X_ROUND, X_TILES)):
+                for i in range(x_done, min(x_done + X_HALF[half], X_TILES)):
                     flip_x_tile(i, nc.vector.tensor_copy if i % X_VECTOR == X_VECTOR - 1 else nc.scalar.copy)
-                x_done = min(x_done + X_ROUND, X_TILES)
-                flip_e(b)
-                quantise_e(b)
-                if b + 1 < B:
-                    exponentials(b + 1)
-                    values(b + 1)
-                outputs(b)
-                if b + 1 < B:
-                    quantise_v(b + 1)
+                x_done = min(x_done + X_HALF[half], X_TILES)
+                if 0 <= b + 1 < B:
+                    flip_e(b + 1, half)
+                if 0 <= b + V_LEAD < B:
+                    values(b + V_LEAD, half)
+                out_b, out_half = (step - 1) // 2, (step - 1) % 2
+                if 0 <= out_b < B:
+                    outputs(out_b, out_half)
+                    pending = [(out_b, out_half)]
+                if 0 <= b + 2 < B:
+                    exponentials(b + 2, half)

@@ -25,14 +25,24 @@ X_BUFS = 2
 QK_BUFS = 4
 X_TILES = B * 2 * TILES
 X_EARLY = 28
-X_START = 4
+X_START = 3
 X_HALF = (3, 3)
 V_LEAD = 2
 ROOT_ROWS = 2
+SCORE_BANKS = 4
+VALUE_BANKS = 2
+OUTPUT_BANKS = 1
+SCALAR_FROM = 8
+SCALAR_HALF = 0
+O_BUFS = 3
+QE_HALF = 0
+X_FIRST = 0
+V_FIRST = 0
+W_STEP = 1
 FLIP_AT = 1
-W_AT = 8
-MAX_LAG = 12
-X_VECTOR = 3
+W_AT = 9
+MAX_LAG = 6
+X_VECTOR = 2
 HALVES = ((0, 1), (2, 3))
 
 FLOPS = 4 * 2 * B * S * DX * HD + 4 * 2 * B * S * S * HD + 2 * 2 * B * S * S * HD
@@ -58,8 +68,7 @@ def tile_covenantattention_pa_t_kernel(
         x_pool = whole.enter_context(tc.tile_pool(name="x_pool", bufs=X_BUFS))
         x_keep = whole.enter_context(tc.tile_pool(name="x_keep", bufs=5))
         x_stage = whole.enter_context(tc.tile_pool(name="x_stage", bufs=3))
-        mm_psum = whole.enter_context(tc.psum_pool(name="mm_psum", bufs=4))
-        tr_psum = whole.enter_context(tc.psum_pool(name="tr_psum", bufs=4))
+        psum = {}
 
         warm = const.tile([P, 1], F32)
         nc.vector.memset(warm[:], 1.0)
@@ -95,7 +104,7 @@ def tile_covenantattention_pa_t_kernel(
                 x_words[(b, part)] = x_stage.tile(
                     [P, TILES, PASSES, P, PACK], BF16, align_bytes=64, name="x_grouped", tag="x_grouped"
                 )
-            bank = tr_psum.tile([P, BLOCKS, P], F32, name="bank", tag="bank")
+            bank = psum["flips"].tile([P, BLOCKS, P], F32, name="bank", tag="bank")
             transpose_words(nc, bank, x_nat[(b, part)][:, t, :], ident_f32)
             copy(
                 out=x_words[(b, part)][:, t].bitcast(F32),
@@ -118,21 +127,22 @@ def tile_covenantattention_pa_t_kernel(
             )
             x_mx[(b, part)] = (x_codes, x_scales)
 
-        def quantise_weights():
-            nc.vector.tensor_scalar_mul(out=w_nat[:, W_NEG_I, :], in0=w_nat[:, W_I, :], scalar1=-1.0)
-            for w in range(3):
-                bank = tr_psum.tile([P, BLOCKS, P], F32, name="bank", tag="bank")
-                transpose_words(nc, bank, w_nat[:, w, :], ident_f32)
-                nc.vector.tensor_copy(
-                    out=w_grouped[:, w].bitcast(F32),
-                    in_=bank[:].rearrange("p (g u) d -> p g d u", u=2),
+        def quantise_weight(w):
+            if w == W_R:
+                nc.gpsimd.tensor_scalar(
+                    out=w_nat[:, W_NEG_I, :], in0=w_nat[:, W_I, :], scalar1=-1.0, scalar2=0.0, op0=ALU.mult, op1=ALU.add
                 )
-            for w in range(3):
-                nc.vector.quantize_mx(
-                    out=w_codes[:, w].rearrange("p g d -> p (g d)").bitcast(FP8X4),
-                    scales=w_scales[:, w].rearrange("p g d -> p (g d)"),
-                    in_=w_grouped[:, w].rearrange("p g d j -> p (g d j)"),
-                )
+            bank = psum["flips"].tile([P, BLOCKS, P], F32, name="bank", tag="bank")
+            transpose_words(nc, bank, w_nat[:, w, :], ident_f32)
+            nc.vector.tensor_copy(
+                out=w_grouped[:, w].bitcast(F32),
+                in_=bank[:].rearrange("p (g u) d -> p g d u", u=2),
+            )
+            nc.vector.quantize_mx(
+                out=w_codes[:, w].rearrange("p g d -> p (g d)").bitcast(FP8X4),
+                scales=w_scales[:, w].rearrange("p g d -> p (g d)"),
+                in_=w_grouped[:, w].rearrange("p g d j -> p (g d j)"),
+            )
 
         def magnitudes(row):
             b, j = row // TILES, row % TILES
@@ -140,15 +150,18 @@ def tile_covenantattention_pa_t_kernel(
             nc.scalar.activation(out=flat, in_=flat, func=ACT.Sqrt, scale=1.0 / HD)
 
         def negated_row_max(row):
+            j = row % TILES
             nc.vector.tensor_reduce(
-                out=neg_max[:, row : row + 1],
-                in_=m_tiles[row // TILES][:, row % TILES, :],
+                out=neg_max[:, row : row + 2],
+                in_=m_tiles[row // TILES][:, j : j + 2, :],
                 axis=AXIS.X,
                 op=ALU.max,
                 negate=True,
             )
 
         with ExitStack() as phase:
+            psum["scores"] = phase.enter_context(tc.psum_pool(name="score_psum", bufs=SCORE_BANKS))
+            psum["flips"] = phase.enter_context(tc.psum_pool(name="flip_psum", bufs=8 - SCORE_BANKS))
             nat = phase.enter_context(tc.tile_pool(name="nat", bufs=QK_BUFS))
             flipped = phase.enter_context(tc.tile_pool(name="flipped", bufs=3))
             squares = phase.enter_context(tc.tile_pool(name="squares", bufs=3))
@@ -171,8 +184,8 @@ def tile_covenantattention_pa_t_kernel(
 
             def flip_qk(b):
                 q_nat, k_nat = qk_nat[b]
-                q_ps = tr_psum.tile([P, 2, TILES, P], BF16, name="bank", tag="bank")
-                k_ps = tr_psum.tile([P, 2, TILES, P], BF16, name="bank", tag="bank")
+                q_ps = psum["flips"].tile([P, 2, TILES, P], BF16, name="bank", tag="bank")
+                k_ps = psum["flips"].tile([P, 2, TILES, P], BF16, name="bank", tag="bank")
                 for part in (REAL, IMAG):
                     for j in range(TILES):
                         nc.tensor.transpose(q_ps[:, part, j, :], q_nat[:, part, j, :], ident_bf[:])
@@ -200,8 +213,8 @@ def tile_covenantattention_pa_t_kernel(
             def squared_magnitudes(b, j):
                 q_t, neg_qi_t, k_t = qk_t[b]
                 cols = slice(j * P, (j + 1) * P)
-                s_r = mm_psum.tile([P, S], F32, name="bank", tag="bank")
-                s_i = mm_psum.tile([P, S], F32, name="bank", tag="bank")
+                s_r = psum["scores"].tile([P, S], F32, name="bank", tag="bank")
+                s_i = psum["scores"].tile([P, S], F32, name="bank", tag="bank")
                 nc.tensor.matmul(s_r[:], lhsT=q_t[:, REAL, cols], rhs=k_t[:, REAL, :], start=True, stop=False)
                 nc.tensor.matmul(s_r[:], lhsT=neg_qi_t[:, cols], rhs=k_t[:, IMAG, :], start=False, stop=True)
                 nc.tensor.matmul(s_i[:], lhsT=q_t[:, REAL, cols], rhs=k_t[:, IMAG, :], start=True, stop=False)
@@ -213,9 +226,12 @@ def tile_covenantattention_pa_t_kernel(
                 nc.gpsimd.tensor_tensor(out=m_row, in0=m_row, in1=sq_i[:], op=ALU.add)
 
             load_qk(0)
+            if X_FIRST:
+                load_x(0, REAL)
             load_qk(1)
-            for part in (REAL, IMAG):
-                load_x(0, part)
+            if not X_FIRST:
+                load_x(0, REAL)
+            load_x(0, IMAG)
             for b in range(2, QK_BUFS):
                 load_qk(b)
             nc.sync.dma_start(out=w_nat[:, W_R, :], in_=wv_r)
@@ -230,14 +246,14 @@ def tile_covenantattention_pa_t_kernel(
                 for j in range(TILES):
                     squared_magnitudes(b, j)
                     step = b * TILES + j
-                    if step >= MAX_LAG:
+                    if step >= MAX_LAG and step % 2 == 0:
                         negated_row_max(step - MAX_LAG)
                     if step > ROOT_ROWS and step % ROOT_ROWS == ROOT_ROWS - 1:
                         magnitudes(step - 2 * ROOT_ROWS + 1)
                     if step % TILES == FLIP_AT and b + 1 < B:
                         flip_qk(b + 1)
-                    if step == W_AT:
-                        quantise_weights()
+                    if W_AT <= step < W_AT + 3 * W_STEP and (step - W_AT) % W_STEP == 0:
+                        quantise_weight((step - W_AT) // W_STEP)
                     x_tile = step - X_START
                     if 0 <= x_tile < X_EARLY:
                         flip_x_tile(x_tile, nc.vector.tensor_copy)
@@ -249,10 +265,16 @@ def tile_covenantattention_pa_t_kernel(
             magnitudes(B * TILES - ROOT_ROWS)
 
         with ExitStack() as era:
+            psum["values"] = era.enter_context(tc.psum_pool(name="value_psum", bufs=VALUE_BANKS))
+            psum["outputs"] = era.enter_context(tc.psum_pool(name="output_psum", bufs=OUTPUT_BANKS))
+            psum["flips"] = era.enter_context(
+                tc.psum_pool(name="late_flip_psum", bufs=8 - VALUE_BANKS - OUTPUT_BANKS)
+            )
             stage = era.enter_context(tc.tile_pool(name="stage", bufs=2, reuse_waits="tile"))
 
             e_pool = era.enter_context(tc.tile_pool(name="e_pool", bufs=3, reuse_waits="tile"))
 
+            o_pool = era.enter_context(tc.tile_pool(name="o_pool", bufs=O_BUFS, reuse_waits="tile"))
             e_rows = {}
             e_words = {}
             e_mx = {}
@@ -281,7 +303,7 @@ def tile_covenantattention_pa_t_kernel(
                     e_words[b] = stage.tile(
                         [P, TILES, P, PACK], BF16, align_bytes=64, name="e_grouped", tag="e_grouped"
                     )
-                bank = tr_psum.tile([P, 2, 2, P], F32, name="bank", tag="bank")
+                bank = psum["flips"].tile([P, 2, 2, P], F32, name="bank", tag="bank")
                 for jj in range(2):
                     transpose_words(nc, bank[:, jj], e_rows[b][:, 2 * half + jj, :], ident_f32)
                 nc.scalar.copy(
@@ -302,7 +324,7 @@ def tile_covenantattention_pa_t_kernel(
             def values(b, half):
                 if half == 0:
                     v_banks[b] = [
-                        mm_psum.tile([P, TILES, HD], F32, name="bank", tag="bank") for part in (REAL, IMAG)
+                        psum["values"].tile([P, TILES, HD], F32, name="bank", tag="bank") for part in (REAL, IMAG)
                     ]
                 steps = [(part, g) for part in (REAL, IMAG) for g in range(PASSES)]
                 for t in HALVES[half]:
@@ -348,8 +370,8 @@ def tile_covenantattention_pa_t_kernel(
                 if half == 0:
                     cols_b = slice(b * TILES, (b + 1) * TILES)
                     nc.vector.reciprocal(out=inv_sum[:, cols_b], in_=row_sum[:, cols_b])
-                    o_tiles[b] = stage.tile([P, 2, TILES, HD], F32, name="o_sb", tag="o_sb")
-                o_ps = mm_psum.tile([P, 2, 2 * HD], F32, name="bank", tag="bank")
+                    o_tiles[b] = o_pool.tile([P, 2, TILES, HD], F32, name="o_sb", tag="o_sb")
+                o_ps = psum["outputs"].tile([P, 2, 2 * HD], F32, name="bank", tag="bank")
                 o_banks[b, half] = o_ps
                 for jj, j in enumerate(HALVES[half]):
                     cols = slice(j * P, (j + 1) * P)
@@ -366,12 +388,22 @@ def tile_covenantattention_pa_t_kernel(
             def normalise(b, half):
                 o_sb = o_tiles[b]
                 o_ps = o_banks[b, half]
-                for jj, j in enumerate(HALVES[half]):
-                    col = b * TILES + j
-                    nc.vector.tensor_scalar_mul(
-                        out=o_sb[:, :, j, :],
-                        in0=o_ps[:, jj, :].rearrange("p (c d) -> p c d", c=2),
-                        scalar1=inv_sum[:, col : col + 1],
+                if half >= SCALAR_HALF or b >= SCALAR_FROM:
+                    for jj, j in enumerate(HALVES[half]):
+                        col = b * TILES + j
+                        nc.scalar.activation(
+                            out=o_sb[:, :, j, :],
+                            in_=o_ps[:, jj, :].rearrange("p (c d) -> p c d", c=2),
+                            func=ACT.Copy,
+                            scale=inv_sum[:, col : col + 1],
+                        )
+                else:
+                    col = b * TILES + 2 * half
+                    nc.vector.tensor_tensor(
+                        out=o_sb[:, :, 2 * half : 2 * half + 2, :].rearrange("p c j d -> p j c d"),
+                        in0=o_ps[:].rearrange("p j (c d) -> p j c d", c=2),
+                        in1=inv_sum[:, col : col + 2].unsqueeze(2).unsqueeze(3).to_broadcast([P, 2, 2, HD]),
+                        op=ALU.mult,
                     )
                 if half == 1:
                     for part in (REAL, IMAG):
@@ -385,9 +417,9 @@ def tile_covenantattention_pa_t_kernel(
                 for done in pending:
                     normalise(*done)
                 pending = []
-                for row in range(B * TILES - MAX_LAG + 2 * (step + 4), B * TILES - MAX_LAG + 2 * (step + 5)):
-                    if row < B * TILES:
-                        negated_row_max(row)
+                row = B * TILES - MAX_LAG + 2 * (step + 4)
+                if row < B * TILES:
+                    negated_row_max(row)
                 if half == 0:
                     if 0 <= b - 1 + V_LEAD < B:
                         biased_values(b - 1 + V_LEAD)
@@ -399,7 +431,8 @@ def tile_covenantattention_pa_t_kernel(
                     quantise_x(groups_done // 2, groups_done % 2)
                     groups_done += 1
                 for i in range(x_done, min(x_done + X_HALF[half], X_TILES)):
-                    flip_x_tile(i, nc.vector.tensor_copy if i % X_VECTOR == X_VECTOR - 1 else nc.scalar.copy)
+                    on_vector = i < X_EARLY + V_FIRST or i % X_VECTOR == X_VECTOR - 1
+                    flip_x_tile(i, nc.vector.tensor_copy if on_vector else nc.scalar.copy)
                 x_done = min(x_done + X_HALF[half], X_TILES)
                 if 0 <= b + 1 < B:
                     flip_e(b + 1, half)

@@ -29,11 +29,12 @@ X_START = 3
 X_HALF = (3, 3)
 V_LEAD = 2
 ROOT_ROWS = 2
+FLIP_BANKS = 4
 SCORE_BANKS = 4
 VALUE_BANKS = 2
-OUTPUT_BANKS = 1
-SCALAR_FROM = 8
-SCALAR_HALF = 0
+OUTPUT_BANKS = 2
+NORM_VECTOR = 7
+E_VECTOR = 5
 O_BUFS = 3
 QE_HALF = 0
 X_FIRST = 0
@@ -68,7 +69,7 @@ def tile_covenantattention_pa_t_kernel(
         x_pool = whole.enter_context(tc.tile_pool(name="x_pool", bufs=X_BUFS))
         x_keep = whole.enter_context(tc.tile_pool(name="x_keep", bufs=5))
         x_stage = whole.enter_context(tc.tile_pool(name="x_stage", bufs=3))
-        psum = {}
+        psum = {"flips": whole.enter_context(tc.psum_pool(name="flip_psum", bufs=FLIP_BANKS))}
 
         warm = const.tile([P, 1], F32)
         nc.vector.memset(warm[:], 1.0)
@@ -161,7 +162,6 @@ def tile_covenantattention_pa_t_kernel(
 
         with ExitStack() as phase:
             psum["scores"] = phase.enter_context(tc.psum_pool(name="score_psum", bufs=SCORE_BANKS))
-            psum["flips"] = phase.enter_context(tc.psum_pool(name="flip_psum", bufs=8 - SCORE_BANKS))
             nat = phase.enter_context(tc.tile_pool(name="nat", bufs=QK_BUFS))
             flipped = phase.enter_context(tc.tile_pool(name="flipped", bufs=3))
             squares = phase.enter_context(tc.tile_pool(name="squares", bufs=3))
@@ -265,11 +265,8 @@ def tile_covenantattention_pa_t_kernel(
             magnitudes(B * TILES - ROOT_ROWS)
 
         with ExitStack() as era:
-            psum["values"] = era.enter_context(tc.psum_pool(name="value_psum", bufs=VALUE_BANKS))
-            psum["outputs"] = era.enter_context(tc.psum_pool(name="output_psum", bufs=OUTPUT_BANKS))
-            psum["flips"] = era.enter_context(
-                tc.psum_pool(name="late_flip_psum", bufs=8 - VALUE_BANKS - OUTPUT_BANKS)
-            )
+            psum["values"] = era.enter_context(tc.psum_pool(name="value_psum", bufs=VALUE_BANKS, reuse_waits="tile"))
+            psum["outputs"] = era.enter_context(tc.psum_pool(name="output_psum", bufs=OUTPUT_BANKS, reuse_waits="tile"))
             stage = era.enter_context(tc.tile_pool(name="stage", bufs=2, reuse_waits="tile"))
 
             e_pool = era.enter_context(tc.tile_pool(name="e_pool", bufs=3, reuse_waits="tile"))
@@ -306,7 +303,8 @@ def tile_covenantattention_pa_t_kernel(
                 bank = psum["flips"].tile([P, 2, 2, P], F32, name="bank", tag="bank")
                 for jj in range(2):
                     transpose_words(nc, bank[:, jj], e_rows[b][:, 2 * half + jj, :], ident_f32)
-                nc.scalar.copy(
+                copy = nc.vector.tensor_copy if b >= E_VECTOR and half == 1 else nc.scalar.copy
+                copy(
                     out=e_words[b][:, 2 * half : 2 * half + 2].bitcast(F32),
                     in_=bank[:].rearrange("p j u q -> p j q u"),
                 )
@@ -321,38 +319,36 @@ def tile_covenantattention_pa_t_kernel(
                 )
                 e_mx[b] = (e_codes, e_scales)
 
-            def values(b, half):
-                if half == 0:
-                    v_banks[b] = [
-                        psum["values"].tile([P, TILES, HD], F32, name="bank", tag="bank") for part in (REAL, IMAG)
-                    ]
-                steps = [(part, g) for part in (REAL, IMAG) for g in range(PASSES)]
-                for t in HALVES[half]:
+            def values(b, v_part):
+                bank = psum["values"].tile([P, TILES, HD], F32, name="bank", tag="bank")
+                v_banks[b, v_part] = bank
+                steps = [(x_part, g) for x_part in (REAL, IMAG) for g in range(PASSES)]
+                for t in range(TILES):
                     for n, (x_part, g) in enumerate(steps):
                         x_codes, x_scales = x_mx[(b, x_part)]
                         cols = slice((t * PASSES + g) * P, (t * PASSES + g + 1) * P)
-                        for v_part in (REAL, IMAG):
-                            w = WEIGHT_OF[x_part][v_part]
-                            nc.tensor.matmul_mx(
-                                out=v_banks[b][v_part][:, t, :],
-                                lhsT=x_codes[:, cols].bitcast(FP8X4),
-                                lhsT_scale=x_scales[:, cols],
-                                rhs=w_codes[:, w, g, :].bitcast(FP8X4),
-                                rhs_scale=w_scales[:, w, g, :],
-                                start=(n == 0),
-                                stop=(n == len(steps) - 1),
-                            )
+                        w = WEIGHT_OF[x_part][v_part]
+                        nc.tensor.matmul_mx(
+                            out=bank[:, t, :],
+                            lhsT=x_codes[:, cols].bitcast(FP8X4),
+                            lhsT_scale=x_scales[:, cols],
+                            rhs=w_codes[:, w, g, :].bitcast(FP8X4),
+                            rhs_scale=w_scales[:, w, g, :],
+                            start=(n == 0),
+                            stop=(n == len(steps) - 1),
+                        )
 
-            def biased_values(b):
-                v_grouped = stage.tile([P, 2, HD, PACK], BF16, align_bytes=64)
-                for v_part in (REAL, IMAG):
-                    nc.vector.tensor_tensor(
-                        out=v_grouped[:, v_part],
-                        in0=v_banks[b][v_part][:].rearrange("p t d -> p d t"),
-                        in1=bias[:, v_part, :].unsqueeze(2).to_broadcast([P, HD, PACK]),
-                        op=ALU.add,
+            def biased_values(b, v_part):
+                if v_part == REAL:
+                    v_words[b] = stage.tile(
+                        [P, 2, HD, PACK], BF16, align_bytes=64, name="v_grouped", tag="v_grouped"
                     )
-                v_words[b] = v_grouped
+                nc.vector.tensor_tensor(
+                    out=v_words[b][:, v_part],
+                    in0=v_banks[b, v_part][:].rearrange("p t d -> p d t"),
+                    in1=bias[:, v_part, :].unsqueeze(2).to_broadcast([P, HD, PACK]),
+                    op=ALU.add,
+                )
 
             def quantise_v(b):
                 v_codes = e_pool.tile([P, 2 * HD], U32, align_bytes=64)
@@ -388,7 +384,7 @@ def tile_covenantattention_pa_t_kernel(
             def normalise(b, half):
                 o_sb = o_tiles[b]
                 o_ps = o_banks[b, half]
-                if half >= SCALAR_HALF or b >= SCALAR_FROM:
+                if b < NORM_VECTOR:
                     for jj, j in enumerate(HALVES[half]):
                         col = b * TILES + j
                         nc.scalar.activation(
@@ -422,11 +418,14 @@ def tile_covenantattention_pa_t_kernel(
                     negated_row_max(row)
                 if half == 0:
                     if 0 <= b - 1 + V_LEAD < B:
-                        biased_values(b - 1 + V_LEAD)
+                        biased_values(b - 1 + V_LEAD, IMAG)
                     if 0 <= b < B:
                         quantise_e(b)
-                elif 0 <= b - 1 + V_LEAD < B:
-                    quantise_v(b - 1 + V_LEAD)
+                else:
+                    if 0 <= b + V_LEAD < B:
+                        biased_values(b + V_LEAD, REAL)
+                    if 0 <= b - 1 + V_LEAD < B:
+                        quantise_v(b - 1 + V_LEAD)
                 while groups_done < x_done // TILES:
                     quantise_x(groups_done // 2, groups_done % 2)
                     groups_done += 1

@@ -35,11 +35,12 @@ VALUE_BANKS = 2
 OUTPUT_BANKS = 2
 NORM_VECTOR = 7
 E_VECTOR = 5
-O_BUFS = 3
+O_BUFS = 6
 QE_HALF = 0
 X_FIRST = 0
 V_FIRST = 0
 W_STEP = 1
+WARM_UP = 3
 FLIP_AT = 1
 W_AT = 9
 MAX_LAG = 6
@@ -225,6 +226,12 @@ def tile_covenantattention_pa_t_kernel(
                 nc.scalar.activation(out=sq_i[:], in_=s_i[:], func=ACT.Square)
                 nc.gpsimd.tensor_tensor(out=m_row, in0=m_row, in1=sq_i[:], op=ALU.add)
 
+            zeros = const.tile([P, S], BF16)
+            nc.vector.memset(zeros[:], 0.0)
+            idle = psum["scores"].tile([P, S], F32, name="bank", tag="bank")
+            for i in range(WARM_UP):
+                nc.tensor.matmul(idle[:], lhsT=zeros[:, :P], rhs=zeros[:], start=True, stop=True)
+
             load_qk(0)
             if X_FIRST:
                 load_x(0, REAL)
@@ -262,7 +269,6 @@ def tile_covenantattention_pa_t_kernel(
                         quantise_x(group // 2, group % 2)
             x_done = X_EARLY
             groups_done = x_done // TILES - 1
-            magnitudes(B * TILES - ROOT_ROWS)
 
         with ExitStack() as era:
             psum["values"] = era.enter_context(tc.psum_pool(name="value_psum", bufs=VALUE_BANKS, reuse_waits="tile"))
@@ -279,7 +285,6 @@ def tile_covenantattention_pa_t_kernel(
             v_words = {}
             v_mx = {}
 
-            o_tiles = {}
             o_banks = {}
 
             def exponentials(b, half):
@@ -366,7 +371,6 @@ def tile_covenantattention_pa_t_kernel(
                 if half == 0:
                     cols_b = slice(b * TILES, (b + 1) * TILES)
                     nc.vector.reciprocal(out=inv_sum[:, cols_b], in_=row_sum[:, cols_b])
-                    o_tiles[b] = o_pool.tile([P, 2, TILES, HD], F32, name="o_sb", tag="o_sb")
                 o_ps = psum["outputs"].tile([P, 2, 2 * HD], F32, name="bank", tag="bank")
                 o_banks[b, half] = o_ps
                 for jj, j in enumerate(HALVES[half]):
@@ -382,13 +386,13 @@ def tile_covenantattention_pa_t_kernel(
                     )
 
             def normalise(b, half):
-                o_sb = o_tiles[b]
+                o_sb = o_pool.tile([P, 2, 2, HD], F32)
                 o_ps = o_banks[b, half]
                 if b < NORM_VECTOR:
                     for jj, j in enumerate(HALVES[half]):
                         col = b * TILES + j
                         nc.scalar.activation(
-                            out=o_sb[:, :, j, :],
+                            out=o_sb[:, :, jj, :],
                             in_=o_ps[:, jj, :].rearrange("p (c d) -> p c d", c=2),
                             func=ACT.Copy,
                             scale=inv_sum[:, col : col + 1],
@@ -396,16 +400,16 @@ def tile_covenantattention_pa_t_kernel(
                 else:
                     col = b * TILES + 2 * half
                     nc.vector.tensor_tensor(
-                        out=o_sb[:, :, 2 * half : 2 * half + 2, :].rearrange("p c j d -> p j c d"),
+                        out=o_sb[:].rearrange("p c j d -> p j c d"),
                         in0=o_ps[:].rearrange("p j (c d) -> p j c d", c=2),
                         in1=inv_sum[:, col : col + 2].unsqueeze(2).unsqueeze(3).to_broadcast([P, 2, 2, HD]),
                         op=ALU.mult,
                     )
-                if half == 1:
-                    for part in (REAL, IMAG):
-                        nc.sync.dma_start(
-                            out=outs[part][b].rearrange("(p j) d -> p j d", j=TILES), in_=o_sb[:, part]
-                        )
+                rows = slice(2 * half, 2 * half + 2)
+                for part in (REAL, IMAG):
+                    nc.sync.dma_start(
+                        out=outs[part][b].rearrange("(p j) d -> p j d", j=TILES)[:, rows], in_=o_sb[:, part]
+                    )
 
             pending = []
             for step in range(-4, 2 * B + 2):
@@ -426,13 +430,16 @@ def tile_covenantattention_pa_t_kernel(
                         biased_values(b + V_LEAD, REAL)
                     if 0 <= b - 1 + V_LEAD < B:
                         quantise_v(b - 1 + V_LEAD)
-                while groups_done < x_done // TILES:
-                    quantise_x(groups_done // 2, groups_done % 2)
-                    groups_done += 1
+                x_before = x_done
                 for i in range(x_done, min(x_done + X_HALF[half], X_TILES)):
                     on_vector = i < X_EARLY + V_FIRST or i % X_VECTOR == X_VECTOR - 1
                     flip_x_tile(i, nc.vector.tensor_copy if on_vector else nc.scalar.copy)
                 x_done = min(x_done + X_HALF[half], X_TILES)
+                while groups_done < x_before // TILES:
+                    quantise_x(groups_done // 2, groups_done % 2)
+                    groups_done += 1
+                if step == -2 * V_LEAD:
+                    magnitudes(B * TILES - ROOT_ROWS)
                 if 0 <= b + 1 < B:
                     flip_e(b + 1, half)
                 if 0 <= b + V_LEAD < B:

@@ -34,7 +34,7 @@ SCORE_BANKS = 4
 VALUE_BANKS = 2
 OUTPUT_BANKS = 2
 NORM_VECTOR = 7
-E_VECTOR = 5
+E_VECTOR = 4
 O_BUFS = 6
 QE_HALF = 0
 X_FIRST = 0
@@ -42,7 +42,7 @@ V_FIRST = 0
 W_STEP = 1
 WARM_UP = 3
 FLIP_AT = 1
-W_AT = 9
+W_AT = 5
 MAX_LAG = 6
 X_VECTOR = 2
 HALVES = ((0, 1), (2, 3))
@@ -86,7 +86,7 @@ def tile_covenantattention_pa_t_kernel(
         inv_sum = const.tile([P, B * TILES], F32)
         m_tiles = [m_pool.tile([P, TILES, S], F32, name="m%d" % b) for b in range(B)]
 
-        w_nat = const.tile([P, 3, DX], BF16)
+        w_nat = const.tile([P, 2, DX], BF16)
         bias = const.tile([P, 2, HD], BF16)
         w_grouped = const.tile([P, 3, PASSES, HD, PACK], BF16, align_bytes=64)
         w_codes = const.tile([P, 3, PASSES, HD], U32, align_bytes=64)
@@ -130,16 +130,19 @@ def tile_covenantattention_pa_t_kernel(
             x_mx[(b, part)] = (x_codes, x_scales)
 
         def quantise_weight(w):
-            if w == W_R:
-                nc.gpsimd.tensor_scalar(
-                    out=w_nat[:, W_NEG_I, :], in0=w_nat[:, W_I, :], scalar1=-1.0, scalar2=0.0, op0=ALU.mult, op1=ALU.add
+            if w == W_NEG_I:
+                nc.vector.tensor_scalar_mul(
+                    out=w_grouped[:, w].rearrange("p g d j -> p (g d j)"),
+                    in0=w_grouped[:, W_I].rearrange("p g d j -> p (g d j)"),
+                    scalar1=-1.0,
                 )
-            bank = psum["flips"].tile([P, BLOCKS, P], F32, name="bank", tag="bank")
-            transpose_words(nc, bank, w_nat[:, w, :], ident_f32)
-            nc.vector.tensor_copy(
-                out=w_grouped[:, w].bitcast(F32),
-                in_=bank[:].rearrange("p (g u) d -> p g d u", u=2),
-            )
+            else:
+                bank = psum["flips"].tile([P, BLOCKS, P], F32, name="bank", tag="bank")
+                transpose_words(nc, bank, w_nat[:, w, :], ident_f32)
+                nc.vector.tensor_copy(
+                    out=w_grouped[:, w].bitcast(F32),
+                    in_=bank[:].rearrange("p (g u) d -> p g d u", u=2),
+                )
             nc.vector.quantize_mx(
                 out=w_codes[:, w].rearrange("p g d -> p (g d)").bitcast(FP8X4),
                 scales=w_scales[:, w].rearrange("p g d -> p (g d)"),
@@ -204,8 +207,8 @@ def tile_covenantattention_pa_t_kernel(
                     out=neg_qi_t[:], in0=q_t[:, IMAG, :], scalar1=-1.0, scalar2=0.0, op0=ALU.mult, op1=ALU.add
                 )
                 nc.vector.tensor_copy(
-                    out=k_t[:].rearrange("d c (u p e) -> d (c u) p e", u=2, e=2),
-                    in_=k_ps[:].rearrange("d c (u e) p -> d (c u) p e", e=2),
+                    out=k_t[:].rearrange("d c s -> d (c s)"),
+                    in_=k_ps[:].rearrange("d c t p -> d (c t p)"),
                 )
                 qk_t[b] = (q_t, neg_qi_t, k_t)
                 if b + QK_BUFS < B:
@@ -214,16 +217,16 @@ def tile_covenantattention_pa_t_kernel(
             def squared_magnitudes(b, j):
                 q_t, neg_qi_t, k_t = qk_t[b]
                 cols = slice(j * P, (j + 1) * P)
-                s_r = psum["scores"].tile([P, S], F32, name="bank", tag="bank")
                 s_i = psum["scores"].tile([P, S], F32, name="bank", tag="bank")
-                nc.tensor.matmul(s_r[:], lhsT=q_t[:, REAL, cols], rhs=k_t[:, REAL, :], start=True, stop=False)
-                nc.tensor.matmul(s_r[:], lhsT=neg_qi_t[:, cols], rhs=k_t[:, IMAG, :], start=False, stop=True)
+                s_r = psum["scores"].tile([P, S], F32, name="bank", tag="bank")
                 nc.tensor.matmul(s_i[:], lhsT=q_t[:, REAL, cols], rhs=k_t[:, IMAG, :], start=True, stop=False)
                 nc.tensor.matmul(s_i[:], lhsT=q_t[:, IMAG, cols], rhs=k_t[:, REAL, :], start=False, stop=True)
+                nc.tensor.matmul(s_r[:], lhsT=q_t[:, REAL, cols], rhs=k_t[:, REAL, :], start=True, stop=False)
+                nc.tensor.matmul(s_r[:], lhsT=neg_qi_t[:, cols], rhs=k_t[:, IMAG, :], start=False, stop=True)
                 sq_i = squares.tile([P, S], F32)
                 m_row = m_tiles[b][:, j, :]
-                nc.scalar.activation(out=m_row, in_=s_r[:], func=ACT.Square)
                 nc.scalar.activation(out=sq_i[:], in_=s_i[:], func=ACT.Square)
+                nc.scalar.activation(out=m_row, in_=s_r[:], func=ACT.Square)
                 nc.gpsimd.tensor_tensor(out=m_row, in0=m_row, in1=sq_i[:], op=ALU.add)
 
             zeros = const.tile([P, S], BF16)
@@ -293,8 +296,8 @@ def tile_covenantattention_pa_t_kernel(
                 for j in HALVES[half]:
                     col = b * TILES + j
                     nc.scalar.activation(
-                        out=e_rows[b][:, j, :],
-                        in_=m_tiles[b][:, j, :],
+                        out=e_rows[b][:, j, :].rearrange("p (u k e) -> p u k e", u=2, e=2),
+                        in_=m_tiles[b][:, j, :].rearrange("p (u e k) -> p u k e", u=2, e=2),
                         func=ACT.Exp,
                         bias=neg_max[:, col : col + 1],
                         accum_out=row_sum[:, col : col + 1],

@@ -40,7 +40,7 @@ QE_HALF = 0
 X_FIRST = 0
 V_FIRST = 0
 W_STEP = 1
-WARM_UP = 3
+WARM_UP = 2
 FLIP_AT = 1
 W_AT = 5
 MAX_LAG = 6
@@ -225,8 +225,12 @@ def tile_covenantattention_pa_t_kernel(
                 nc.tensor.matmul(s_r[:], lhsT=neg_qi_t[:, cols], rhs=k_t[:, IMAG, :], start=False, stop=True)
                 sq_i = squares.tile([P, S], F32)
                 m_row = m_tiles[b][:, j, :]
-                nc.scalar.activation(out=sq_i[:], in_=s_i[:], func=ACT.Square)
-                nc.scalar.activation(out=m_row, in_=s_r[:], func=ACT.Square)
+                for square, s in ((sq_i[:], s_i), (m_row, s_r)):
+                    nc.scalar.activation(
+                        out=square.rearrange("p (u k e) -> p u k e", u=2, e=2),
+                        in_=s[:].rearrange("p (u e k) -> p u k e", u=2, e=2),
+                        func=ACT.Square,
+                    )
                 nc.gpsimd.tensor_tensor(out=m_row, in0=m_row, in1=sq_i[:], op=ALU.add)
 
             zeros = const.tile([P, S], BF16)
@@ -296,8 +300,8 @@ def tile_covenantattention_pa_t_kernel(
                 for j in HALVES[half]:
                     col = b * TILES + j
                     nc.scalar.activation(
-                        out=e_rows[b][:, j, :].rearrange("p (u k e) -> p u k e", u=2, e=2),
-                        in_=m_tiles[b][:, j, :].rearrange("p (u e k) -> p u k e", u=2, e=2),
+                        out=e_rows[b][:, j, :],
+                        in_=m_tiles[b][:, j, :],
                         func=ACT.Exp,
                         bias=neg_max[:, col : col + 1],
                         accum_out=row_sum[:, col : col + 1],

@@ -34,15 +34,17 @@ SCORE_BANKS = 4
 VALUE_BANKS = 2
 OUTPUT_BANKS = 2
 NORM_VECTOR = 7
-E_VECTOR = 4
+E_VECTOR = 3
 O_BUFS = 6
 QE_HALF = 0
-X_FIRST = 0
+JOIN_E = 1
+MAX_STEP = -4
+NORM_HALF = 8
 V_FIRST = 0
 W_STEP = 1
 WARM_UP = 2
 FLIP_AT = 1
-W_AT = 5
+W_AT = 4
 MAX_LAG = 6
 X_VECTOR = 2
 HALVES = ((0, 1), (2, 3))
@@ -240,20 +242,17 @@ def tile_covenantattention_pa_t_kernel(
                 nc.tensor.matmul(idle[:], lhsT=zeros[:, :P], rhs=zeros[:], start=True, stop=True)
 
             load_qk(0)
-            if X_FIRST:
-                load_x(0, REAL)
             load_qk(1)
-            if not X_FIRST:
-                load_x(0, REAL)
-            load_x(0, IMAG)
-            for b in range(2, QK_BUFS):
-                load_qk(b)
+            for part in (REAL, IMAG):
+                load_x(0, part)
+            load_qk(2)
             nc.sync.dma_start(out=w_nat[:, W_R, :], in_=wv_r)
             nc.sync.dma_start(out=w_nat[:, W_I, :], in_=wv_i)
-            nc.sync.dma_start(out=bias[:, REAL, :], in_=bv_r.partition_broadcast(P))
-            nc.sync.dma_start(out=bias[:, IMAG, :], in_=bv_i.partition_broadcast(P))
+            load_qk(3)
             for part in (REAL, IMAG):
                 load_x(1, part)
+            nc.sync.dma_start(out=bias[:, REAL, :], in_=bv_r.partition_broadcast(P))
+            nc.sync.dma_start(out=bias[:, IMAG, :], in_=bv_i.partition_broadcast(P))
 
             flip_qk(0)
             for b in range(B):
@@ -395,7 +394,7 @@ def tile_covenantattention_pa_t_kernel(
             def normalise(b, half):
                 o_sb = o_pool.tile([P, 2, 2, HD], F32)
                 o_ps = o_banks[b, half]
-                if b < NORM_VECTOR:
+                if b < NORM_VECTOR and not (b >= NORM_HALF and half == 1):
                     for jj, j in enumerate(HALVES[half]):
                         col = b * TILES + j
                         nc.scalar.activation(
@@ -424,8 +423,8 @@ def tile_covenantattention_pa_t_kernel(
                 for done in pending:
                     normalise(*done)
                 pending = []
-                row = B * TILES - MAX_LAG + 2 * (step + 4)
-                if row < B * TILES:
+                row = B * TILES - MAX_LAG + 2 * (step - MAX_STEP)
+                if B * TILES - MAX_LAG <= row < B * TILES:
                     negated_row_max(row)
                 if half == 0:
                     if 0 <= b - 1 + V_LEAD < B:
@@ -448,7 +447,11 @@ def tile_covenantattention_pa_t_kernel(
                 if step == -2 * V_LEAD:
                     magnitudes(B * TILES - ROOT_ROWS)
                 if 0 <= b + 1 < B:
-                    flip_e(b + 1, half)
+                    if x_before < X_TILES or not JOIN_E:
+                        flip_e(b + 1, half)
+                    elif half == 0:
+                        flip_e(b + 1, 0)
+                        flip_e(b + 1, 1)
                 if 0 <= b + V_LEAD < B:
                     values(b + V_LEAD, half)
                 out_b, out_half = (step - 1) // 2, (step - 1) % 2

from contextlib import ExitStack

import concourse.mybir as mybir
from concourse.masks import make_identity

F32 = mybir.dt.float32
BF16 = mybir.dt.bfloat16
U32 = mybir.dt.uint32
U8 = mybir.dt.uint8
FP8X4 = mybir.dt.float8_e4m3fn_x4
ACT = mybir.ActivationFunctionType
ALU = mybir.AluOpType
AXIS = mybir.AxisListType

P = 128
PACK = 4
B, S, HD, DX = 8, 512, 128, 1024
TILES = S // P
PASSES = DX // (P * PACK)
BLOCKS = DX // (2 * P)
REAL, IMAG = 0, 1
W_R, W_I, W_NEG_I = 0, 1, 2
WEIGHT_OF = ((W_R, W_I), (W_NEG_I, W_R))
X_BUFS = 2
QK_BUFS = 4
X_TILES = B * 2 * TILES
X_EARLY = 28
X_START = 3
X_HALF = (3, 3)
V_LEAD = 2
ROOT_ROWS = 2
FLIP_BANKS = 4
SCORE_BANKS = 4
VALUE_BANKS = 2
OUTPUT_BANKS = 2
NORM_VECTOR = 7
E_VECTOR = 3
O_BUFS = 6
QE_HALF = 0
JOIN_E = 1
MAX_STEP = -4
NORM_HALF = 8
V_FIRST = 0
W_STEP = 1
WARM_UP = 2
FLIP_AT = 1
W_AT = 4
MAX_LAG = 6
X_VECTOR = 2
HALVES = ((0, 1), (2, 3))

FLOPS = 4 * 2 * B * S * DX * HD + 4 * 2 * B * S * S * HD + 2 * 2 * B * S * S * HD


def transpose_words(nc, bank, rows, ident_f32):
    words = rows.bitcast(F32)
    for i in range(bank.shape[1]):
        nc.tensor.transpose(bank[:, i, :], words[:, i * P : (i + 1) * P], ident_f32[:])


def tile_covenantattention_pa_t_kernel(
    tc, x_real, x_imag, q_zeta_r, q_zeta_i, k_zeta_r, k_zeta_i, wv_r, wv_i, bv_r, bv_i, out_0, out_1
):
    nc = tc.nc
    x_parts = (x_real, x_imag)
    outs = (out_0, out_1)

    with ExitStack() as whole:
        whole.enter_context(tc.manual_schedule())
        const = whole.enter_context(tc.tile_pool(name="const", bufs=1))
        m_pool = whole.enter_context(tc.tile_pool(name="m_pool", bufs=1))
        x_pool = whole.enter_context(tc.tile_pool(name="x_pool", bufs=X_BUFS))
        x_keep = whole.enter_context(tc.tile_pool(name="x_keep", bufs=5))
        x_stage = whole.enter_context(tc.tile_pool(name="x_stage", bufs=3))
        psum = {"flips": whole.enter_context(tc.psum_pool(name="flip_psum", bufs=FLIP_BANKS))}

        warm = const.tile([P, 1], F32)
        nc.vector.memset(warm[:], 1.0)
        nc.scalar.activation(out=warm[:], in_=warm[:], func=ACT.Sqrt)

        ident_bf = const.tile([P, P], BF16)
        make_identity(nc, ident_bf[:])
        ident_f32 = const.tile([P, P], F32)
        make_identity(nc, ident_f32[:])

        neg_max = const.tile([P, B * TILES], F32)
        row_sum = const.tile([P, B * TILES], F32)
        inv_sum = const.tile([P, B * TILES], F32)
        m_tiles = [m_pool.tile([P, TILES, S], F32, name="m%d" % b) for b in range(B)]

        w_nat = const.tile([P, 2, DX], BF16)
        bias = const.tile([P, 2, HD], BF16)
        w_grouped = const.tile([P, 3, PASSES, HD, PACK], BF16, align_bytes=64)
        w_codes = const.tile([P, 3, PASSES, HD], U32, align_bytes=64)
        w_scales = const.tile([P, 3, PASSES, HD], U8, align_bytes=64)
        x_nat = {}
        x_words = {}
        x_mx = {}

        def load_x(b, part):
            x_sb = x_pool.tile([P, TILES, DX], BF16, name="x_sb%d" % part, tag="x_sb%d" % part)
            nc.sync.dma_start(out=x_sb[:], in_=x_parts[part][b].rearrange("(p t) f -> p t f", t=TILES))
            x_nat[(b, part)] = x_sb

        def flip_x_tile(i, copy):
            b, part, t = i // (2 * TILES), (i // TILES) % 2, i % TILES
            if t == 0:
                x_words[(b, part)] = x_stage.tile(
                    [P, TILES, PASSES, P, PACK], BF16, align_bytes=64, name="x_grouped", tag="x_grouped"
                )
            bank = psum["flips"].tile([P, BLOCKS, P], F32, name="bank", tag="bank")
            transpose_words(nc, bank, x_nat[(b, part)][:, t, :], ident_f32)
            copy(
                out=x_words[(b, part)][:, t].bitcast(F32),
                in_=bank[:].rearrange("p (g u) k -> p g k u", u=2),
            )
            if t == TILES - 1 and b + X_BUFS < B:
                load_x(b + X_BUFS, part)

        def quantise_x(b, part):
            x_codes = x_keep.tile(
                [P, TILES * PASSES * P], U32, align_bytes=64, name="x_codes%d" % part, tag="x_codes%d" % part
            )
            x_scales = x_keep.tile(
                [P, TILES * PASSES * P], U8, align_bytes=64, name="x_scales%d" % part, tag="x_scales%d" % part
            )
            nc.vector.quantize_mx(
                out=x_codes[:].bitcast(FP8X4),
                scales=x_scales[:],
                in_=x_words[(b, part)][:].rearrange("p t g k j -> p (t g k j)"),
            )
            x_mx[(b, part)] = (x_codes, x_scales)

        def quantise_weight(w):
            if w == W_NEG_I:
                nc.vector.tensor_scalar_mul(
                    out=w_grouped[:, w].rearrange("p g d j -> p (g d j)"),
                    in0=w_grouped[:, W_I].rearrange("p g d j -> p (g d j)"),
                    scalar1=-1.0,
                )
            else:
                bank = psum["flips"].tile([P, BLOCKS, P], F32, name="bank", tag="bank")
                transpose_words(nc, bank, w_nat[:, w, :], ident_f32)
                nc.vector.tensor_copy(
                    out=w_grouped[:, w].bitcast(F32),
                    in_=bank[:].rearrange("p (g u) d -> p g d u", u=2),
                )
            nc.vector.quantize_mx(
                out=w_codes[:, w].rearrange("p g d -> p (g d)").bitcast(FP8X4),
                scales=w_scales[:, w].rearrange("p g d -> p (g d)"),
                in_=w_grouped[:, w].rearrange("p g d j -> p (g d j)"),
            )

        def magnitudes(row):
            b, j = row // TILES, row % TILES
            flat = m_tiles[b][:, j : j + ROOT_ROWS].rearrange("p j s -> p (j s)")
            nc.scalar.activation(out=flat, in_=flat, func=ACT.Sqrt, scale=1.0 / HD)

        def negated_row_max(row):
            j = row % TILES
            nc.vector.tensor_reduce(
                out=neg_max[:, row : row + 2],
                in_=m_tiles[row // TILES][:, j : j + 2, :],
                axis=AXIS.X,
                op=ALU.max,
                negate=True,
            )

        with ExitStack() as phase:
            psum["scores"] = phase.enter_context(tc.psum_pool(name="score_psum", bufs=SCORE_BANKS))
            nat = phase.enter_context(tc.tile_pool(name="nat", bufs=QK_BUFS))
            flipped = phase.enter_context(tc.tile_pool(name="flipped", bufs=3))
            squares = phase.enter_context(tc.tile_pool(name="squares", bufs=3))

            qk_nat = {}
            qk_t = {}

            def load_qk(b):
                q_nat = nat.tile([P, 2, TILES, HD], BF16)
                k_nat = nat.tile([P, 2, TILES, HD], BF16)
                for part, src in ((REAL, q_zeta_r), (IMAG, q_zeta_i)):
                    nc.sync.dma_start(
                        out=q_nat[:, part], in_=src[b, 0].rearrange("(p j) d -> p j d", j=TILES)
                    )
                for part, src in ((REAL, k_zeta_r), (IMAG, k_zeta_i)):
                    nc.sync.dma_start(
                        out=k_nat[:, part], in_=src[b, 0].rearrange("(p t) d -> p t d", t=TILES)
                    )
                qk_nat[b] = (q_nat, k_nat)

            def flip_qk(b):
                q_nat, k_nat = qk_nat[b]
                q_ps = psum["flips"].tile([P, 2, TILES, P], BF16, name="bank", tag="bank")
                k_ps = psum["flips"].tile([P, 2, TILES, P], BF16, name="bank", tag="bank")
                for part in (REAL, IMAG):
                    for j in range(TILES):
                        nc.tensor.transpose(q_ps[:, part, j, :], q_nat[:, part, j, :], ident_bf[:])
                for part in (REAL, IMAG):
                    for t in range(TILES):
                        nc.tensor.transpose(k_ps[:, part, t, :], k_nat[:, part, t, :], ident_bf[:])
                q_t = flipped.tile([P, 2, S], BF16)
                neg_qi_t = flipped.tile([P, S], BF16)
                k_t = flipped.tile([P, 2, S], BF16)
                nc.vector.tensor_copy(
                    out=q_t[:].rearrange("d c s -> d (c s)"),
                    in_=q_ps[:].rearrange("d c j p -> d (c j p)"),
                )
                nc.gpsimd.tensor_scalar(
                    out=neg_qi_t[:], in0=q_t[:, IMAG, :], scalar1=-1.0, scalar2=0.0, op0=ALU.mult, op1=ALU.add
                )
                nc.vector.tensor_copy(
                    out=k_t[:].rearrange("d c s -> d (c s)"),
                    in_=k_ps[:].rearrange("d c t p -> d (c t p)"),
                )
                qk_t[b] = (q_t, neg_qi_t, k_t)
                if b + QK_BUFS < B:
                    load_qk(b + QK_BUFS)

            def squared_magnitudes(b, j):
                q_t, neg_qi_t, k_t = qk_t[b]
                cols = slice(j * P, (j + 1) * P)
                s_i = psum["scores"].tile([P, S], F32, name="bank", tag="bank")
                s_r = psum["scores"].tile([P, S], F32, name="bank", tag="bank")
                nc.tensor.matmul(s_i[:], lhsT=q_t[:, REAL, cols], rhs=k_t[:, IMAG, :], start=True, stop=False)
                nc.tensor.matmul(s_i[:], lhsT=q_t[:, IMAG, cols], rhs=k_t[:, REAL, :], start=False, stop=True)
                nc.tensor.matmul(s_r[:], lhsT=q_t[:, REAL, cols], rhs=k_t[:, REAL, :], start=True, stop=False)
                nc.tensor.matmul(s_r[:], lhsT=neg_qi_t[:, cols], rhs=k_t[:, IMAG, :], start=False, stop=True)
                sq_i = squares.tile([P, S], F32)
                m_row = m_tiles[b][:, j, :]
                for square, s in ((sq_i[:], s_i), (m_row, s_r)):
                    nc.scalar.activation(
                        out=square.rearrange("p (u k e) -> p u k e", u=2, e=2),
                        in_=s[:].rearrange("p (u e k) -> p u k e", u=2, e=2),
                        func=ACT.Square,
                    )
                nc.gpsimd.tensor_tensor(out=m_row, in0=m_row, in1=sq_i[:], op=ALU.add)

            zeros = const.tile([P, S], BF16)
            nc.vector.memset(zeros[:], 0.0)
            idle = psum["scores"].tile([P, S], F32, name="bank", tag="bank")
            for i in range(WARM_UP):
                nc.tensor.matmul(idle[:], lhsT=zeros[:, :P], rhs=zeros[:], start=True, stop=True)

            load_qk(0)
            load_qk(1)
            for part in (REAL, IMAG):
                load_x(0, part)
            load_qk(2)
            nc.sync.dma_start(out=w_nat[:, W_R, :], in_=wv_r)
            nc.sync.dma_start(out=w_nat[:, W_I, :], in_=wv_i)
            load_qk(3)
            for part in (REAL, IMAG):
                load_x(1, part)
            nc.sync.dma_start(out=bias[:, REAL, :], in_=bv_r.partition_broadcast(P))
            nc.sync.dma_start(out=bias[:, IMAG, :], in_=bv_i.partition_broadcast(P))

            flip_qk(0)
            for b in range(B):
                for j in range(TILES):
                    squared_magnitudes(b, j)
                    step = b * TILES + j
                    if step >= MAX_LAG and step % 2 == 0:
                        negated_row_max(step - MAX_LAG)
                    if step > ROOT_ROWS and step % ROOT_ROWS == ROOT_ROWS - 1:
                        magnitudes(step - 2 * ROOT_ROWS + 1)
                    if step % TILES == FLIP_AT and b + 1 < B:
                        flip_qk(b + 1)
                    if W_AT <= step < W_AT + 3 * W_STEP and (step - W_AT) % W_STEP == 0:
                        quantise_weight((step - W_AT) // W_STEP)
                    x_tile = step - X_START
                    if 0 <= x_tile < X_EARLY:
                        flip_x_tile(x_tile, nc.vector.tensor_copy)
                    if TILES <= x_tile < X_EARLY and x_tile % TILES == 1:
                        group = x_tile // TILES - 1
                        quantise_x(group // 2, group % 2)
            x_done = X_EARLY
            groups_done = x_done // TILES - 1

        with ExitStack() as era:
            psum["values"] = era.enter_context(tc.psum_pool(name="value_psum", bufs=VALUE_BANKS, reuse_waits="tile"))
            psum["outputs"] = era.enter_context(tc.psum_pool(name="output_psum", bufs=OUTPUT_BANKS, reuse_waits="tile"))
            stage = era.enter_context(tc.tile_pool(name="stage", bufs=2, reuse_waits="tile"))

            e_pool = era.enter_context(tc.tile_pool(name="e_pool", bufs=3, reuse_waits="tile"))

            o_pool = era.enter_context(tc.tile_pool(name="o_pool", bufs=O_BUFS, reuse_waits="tile"))
            e_rows = {}
            e_words = {}
            e_mx = {}
            v_banks = {}
            v_words = {}
            v_mx = {}

            o_banks = {}

            def exponentials(b, half):
                if half == 0:
                    e_rows[b] = e_pool.tile([P, TILES, S], BF16, name="e_sb", tag="e_sb")
                for j in HALVES[half]:
                    col = b * TILES + j
                    nc.scalar.activation(
                        out=e_rows[b][:, j, :],
                        in_=m_tiles[b][:, j, :],
                        func=ACT.Exp,
                        bias=neg_max[:, col : col + 1],
                        accum_out=row_sum[:, col : col + 1],
                    )

            def flip_e(b, half):
                if half == 0:
                    e_words[b] = stage.tile(
                        [P, TILES, P, PACK], BF16, align_bytes=64, name="e_grouped", tag="e_grouped"
                    )
                bank = psum["flips"].tile([P, 2, 2, P], F32, name="bank", tag="bank")
                for jj in range(2):
                    transpose_words(nc, bank[:, jj], e_rows[b][:, 2 * half + jj, :], ident_f32)
                copy = nc.vector.tensor_copy if b >= E_VECTOR and half == 1 else nc.scalar.copy
                copy(
                    out=e_words[b][:, 2 * half : 2 * half + 2].bitcast(F32),
                    in_=bank[:].rearrange("p j u q -> p j q u"),
                )

            def quantise_e(b):
                e_codes = stage.tile([P, S], U32, align_bytes=64)
                e_scales = stage.tile([P, S], U8, align_bytes=64)
                nc.vector.quantize_mx(
                    out=e_codes[:].bitcast(FP8X4),
                    scales=e_scales[:],
                    in_=e_words[b][:].rearrange("p j q t -> p (j q t)"),
                )
                e_mx[b] = (e_codes, e_scales)

            def values(b, v_part):
                bank = psum["values"].tile([P, TILES, HD], F32, name="bank", tag="bank")
                v_banks[b, v_part] = bank
                steps = [(x_part, g) for x_part in (REAL, IMAG) for g in range(PASSES)]
                for t in range(TILES):
                    for n, (x_part, g) in enumerate(steps):
                        x_codes, x_scales = x_mx[(b, x_part)]
                        cols = slice((t * PASSES + g) * P, (t * PASSES + g + 1) * P)
                        w = WEIGHT_OF[x_part][v_part]
                        nc.tensor.matmul_mx(
                            out=bank[:, t, :],
                            lhsT=x_codes[:, cols].bitcast(FP8X4),
                            lhsT_scale=x_scales[:, cols],
                            rhs=w_codes[:, w, g, :].bitcast(FP8X4),
                            rhs_scale=w_scales[:, w, g, :],
                            start=(n == 0),
                            stop=(n == len(steps) - 1),
                        )

            def biased_values(b, v_part):
                if v_part == REAL:
                    v_words[b] = stage.tile(
                        [P, 2, HD, PACK], BF16, align_bytes=64, name="v_grouped", tag="v_grouped"
                    )
                nc.vector.tensor_tensor(
                    out=v_words[b][:, v_part],
                    in0=v_banks[b, v_part][:].rearrange("p t d -> p d t"),
                    in1=bias[:, v_part, :].unsqueeze(2).to_broadcast([P, HD, PACK]),
                    op=ALU.add,
                )

            def quantise_v(b):
                v_codes = e_pool.tile([P, 2 * HD], U32, align_bytes=64)
                v_scales = e_pool.tile([P, 2 * HD], U8, align_bytes=64)
                nc.vector.quantize_mx(
                    out=v_codes[:].bitcast(FP8X4),
                    scales=v_scales[:],
                    in_=v_words[b][:].rearrange("p c d t -> p (c d t)"),
                )
                v_mx[b] = (v_codes, v_scales)

            def outputs(b, half):
                e_codes, e_scales = e_mx[b]
                v_codes, v_scales = v_mx[b]
                if half == 0:
                    cols_b = slice(b * TILES, (b + 1) * TILES)
                    nc.vector.reciprocal(out=inv_sum[:, cols_b], in_=row_sum[:, cols_b])
                o_ps = psum["outputs"].tile([P, 2, 2 * HD], F32, name="bank", tag="bank")
                o_banks[b, half] = o_ps
                for jj, j in enumerate(HALVES[half]):
                    cols = slice(j * P, (j + 1) * P)
                    nc.tensor.matmul_mx(
                        out=o_ps[:, jj, :],
                        lhsT=e_codes[:, cols].bitcast(FP8X4),
                        lhsT_scale=e_scales[:, cols],
                        rhs=v_codes[:].bitcast(FP8X4),
                        rhs_scale=v_scales[:],
                        start=True,
                        stop=True,
                    )

            def normalise(b, half):
                o_sb = o_pool.tile([P, 2, 2, HD], F32)
                o_ps = o_banks[b, half]
                if b < NORM_VECTOR and not (b >= NORM_HALF and half == 1):
                    for jj, j in enumerate(HALVES[half]):
                        col = b * TILES + j
                        nc.scalar.activation(
                            out=o_sb[:, :, jj, :],
                            in_=o_ps[:, jj, :].rearrange("p (c d) -> p c d", c=2),
                            func=ACT.Copy,
                            scale=inv_sum[:, col : col + 1],
                        )
                else:
                    col = b * TILES + 2 * half
                    nc.vector.tensor_tensor(
                        out=o_sb[:].rearrange("p c j d -> p j c d"),
                        in0=o_ps[:].rearrange("p j (c d) -> p j c d", c=2),
                        in1=inv_sum[:, col : col + 2].unsqueeze(2).unsqueeze(3).to_broadcast([P, 2, 2, HD]),
                        op=ALU.mult,
                    )
                rows = slice(2 * half, 2 * half + 2)
                for part in (REAL, IMAG):
                    nc.sync.dma_start(
                        out=outs[part][b].rearrange("(p j) d -> p j d", j=TILES)[:, rows], in_=o_sb[:, part]
                    )

            pending = []
            for step in range(-4, 2 * B + 2):
                b, half = step // 2, step % 2
                for done in pending:
                    normalise(*done)
                pending = []
                row = B * TILES - MAX_LAG + 2 * (step - MAX_STEP)
                if B * TILES - MAX_LAG <= row < B * TILES:
                    negated_row_max(row)
                if half == 0:
                    if 0 <= b - 1 + V_LEAD < B:
                        biased_values(b - 1 + V_LEAD, IMAG)
                    if 0 <= b < B:
                        quantise_e(b)
                else:
                    if 0 <= b + V_LEAD < B:
                        biased_values(b + V_LEAD, REAL)
                    if 0 <= b - 1 + V_LEAD < B:
                        quantise_v(b - 1 + V_LEAD)
                x_before = x_done
                for i in range(x_done, min(x_done + X_HALF[half], X_TILES)):
                    on_vector = i < X_EARLY + V_FIRST or i % X_VECTOR == X_VECTOR - 1
                    flip_x_tile(i, nc.vector.tensor_copy if on_vector else nc.scalar.copy)
                x_done = min(x_done + X_HALF[half], X_TILES)
                while groups_done < x_before // TILES:
                    quantise_x(groups_done // 2, groups_done % 2)
                    groups_done += 1
                if step == -2 * V_LEAD:
                    magnitudes(B * TILES - ROOT_ROWS)
                if 0 <= b + 1 < B:
                    if x_before < X_TILES or not JOIN_E:
                        flip_e(b + 1, half)
                    elif half == 0:
                        flip_e(b + 1, 0)
                        flip_e(b + 1, 1)
                if 0 <= b + V_LEAD < B:
                    values(b + V_LEAD, half)
                out_b, out_half = (step - 1) // 2, (step - 1) % 2
                if 0 <= out_b < B:
                    outputs(out_b, out_half)
                    pending = [(out_b, out_half)]
                if 0 <= b + 2 < B:
                    exponentials(b + 2, half)
